import numpy as np
import ml_dtypes


def mxq(x, axis, fmt="e4m3"):
    dtype, down = {"e4m3": (ml_dtypes.float8_e4m3fn, 7), "e5m2": (ml_dtypes.float8_e5m2, 14)}[fmt]
    v = np.moveaxis(np.asarray(x, np.float32).astype(ml_dtypes.bfloat16).astype(np.float64), axis, -1)
    blocks = v.reshape(v.shape[:-1] + (-1, 32))
    amax = np.abs(blocks).max(-1, keepdims=True)
    byte = np.maximum(np.where(amax > 0, np.frexp(amax)[1] - 1 + 127, 0) - down, 1)
    scale = np.exp2(byte - 127.0)
    codes = (blocks / scale).astype(np.float32).astype(dtype).astype(np.float64)
    return np.moveaxis((codes * scale).reshape(v.shape), -1, axis)


WIDE = False


def mx_kscale(k):
    if not WIDE:
        return np.ones(k)
    levels = np.array([10, -10, 5, -5, 0])
    a = np.random.permutation(np.resize(levels, k // 512 * 4)).reshape(k // 512, 4)
    idx = np.arange(k)
    return np.exp2(a[idx // 512, idx % 128 // 32])


BF16 = ml_dtypes.bfloat16


def bf(x):
    return np.asarray(x, np.float32).astype(BF16)


def f64(x):
    return np.asarray(x).astype(np.float64)


E2M1 = np.array([0.0, 0.5, 1.0, 1.5, 2.0, 3.0, 4.0, 6.0, -0.0, -0.5, -1.0, -1.5, -2.0, -3.0, -4.0, -6.0])


def pack_weight(w, fmt):
    k, n = w.shape
    w = f64(bf(w)).reshape(k // 32, 32, n)
    amax = np.abs(w).max(1)
    if fmt == "e4m3":
        byte = np.frexp(amax)[1] - 1 + 127 - 7
    else:
        mant, ex = np.frexp(amax / 6.0)
        byte = np.where(mant > 0.5, ex, ex - 1) + 127
    byte = np.clip(np.where(amax > 0, byte, 1), 1, 254)
    scaled = (w * np.exp2(127.0 - byte)[:, None, :]).reshape(k, n).astype(np.float32)
    by_word = np.ascontiguousarray(scaled.reshape(k // 512, 128, 4, n).transpose(0, 1, 3, 2))
    if fmt == "e4m3":
        words = by_word.astype(ml_dtypes.float8_e4m3fn).view(np.uint8)
    else:
        c = by_word.astype(ml_dtypes.float4_e2m1fn).view(np.uint8) & 0xF
        words = c[..., 0::2] | (c[..., 1::2] << 4)
    return np.ascontiguousarray(words), np.ascontiguousarray(byte.astype(np.uint8).reshape(k // 512, 16, n))


def unpack_weight(words, scales, fmt):
    g, p, n, _ = words.shape
    if fmt == "e4m3":
        vals = np.ascontiguousarray(words).view(ml_dtypes.float8_e4m3fn).astype(np.float64)
    else:
        nib = np.empty((g, p, n, 4), np.uint8)
        nib[..., 0::2] = words & 0xF
        nib[..., 1::2] = words >> 4
        vals = E2M1[nib]
    vals = vals * np.repeat(np.exp2(scales.astype(np.float64) - 127.0), 8, axis=1)[..., None]
    return vals.transpose(0, 1, 3, 2).reshape(g * 512, n)


N, D, O, H, W = 6, 512, 128, 32, 32
K = D + D
P = H * W
FMT = "e4m3"


def sigmoid(v):
    return 1.0 / (1.0 + np.exp(-v))


def spatial_gate(re, x_orig):
    a = np.exp(re)
    e = np.exp(a - a.max(1, keepdims=True))
    sm = e / e.sum(1, keepdims=True)
    s = (sm * re).sum(1, keepdims=True)
    return x_orig * s


def setup_inputs():
    t = mx_kscale(D)
    u = t / t.max()
    uc = u[None, :, None, None]
    uu = np.concatenate([u, u])
    x1 = bf(np.random.standard_normal((N, D, H, W)) * 0.5 * uc)
    x2 = bf(np.random.standard_normal((N, D, H, W)) * 0.5 * uc)
    FE_x1 = bf(np.random.standard_normal((N, D, H, W)) * 0.5 * uc)
    FE_x2 = bf(np.random.standard_normal((N, D, H, W)) * 0.5 * uc)
    g1 = bf(np.random.standard_normal((N, D)) * 1.2)
    g2 = bf(np.random.standard_normal((N, D)) * 1.2)
    p1_w_words, p1_w_scales = pack_weight(np.ascontiguousarray((np.random.standard_normal((O, K)) / np.sqrt(K) / uu).T), FMT)
    p1_b = bf(np.random.standard_normal(O) * 0.3)
    p2_w_words, p2_w_scales = pack_weight(np.ascontiguousarray((np.random.standard_normal((O, K)) / np.sqrt(K) / uu).T), FMT)
    p2_b = bf(np.random.standard_normal(O) * 0.3)
    return {"x1": x1, "x2": x2, "FE_x1": FE_x1, "FE_x2": FE_x2, "g1": g1, "g2": g2,
            "p1_w_words": p1_w_words, "p1_w_scales": p1_w_scales, "p1_b": p1_b,
            "p2_w_words": p2_w_words, "p2_w_scales": p2_w_scales, "p2_b": p2_b}


def reference(x1, x2, FE_x1, FE_x2, g1, g2, p1_w_words, p1_w_scales, p1_b, p2_w_words, p2_w_scales, p2_b):
    a1 = f64(x1).reshape(N, D, P)
    a2 = f64(x2).reshape(N, D, P)
    re_x1 = a1 * sigmoid(f64(g1))[:, :, None] + a2
    re_x2 = a2 * sigmoid(f64(g2))[:, :, None] + a1
    fg_x1_sp = spatial_gate(re_x1, a1) + a2
    fg_x2_sp = spatial_gate(re_x2, a2) + a1
    co_x1 = fg_x1_sp + f64(FE_x1).reshape(N, D, P)
    co_x2 = fg_x2_sp + f64(FE_x2).reshape(N, D, P)
    re = np.concatenate([co_x1, co_x2], axis=1)
    rq = mxq(re, 1, "e4m3")
    po_x1 = (unpack_weight(p1_w_words, p1_w_scales, FMT).T @ rq) + f64(p1_b)[None, :, None]
    po_x2 = (unpack_weight(p2_w_words, p2_w_scales, FMT).T @ rq) + f64(p2_b)[None, :, None]
    return po_x1.reshape(N, O, H, W), po_x2.reshape(N, O, H, W)

@@ -1,0 +1,305 @@
+from contextlib import ExitStack
+
+import concourse.mybir as mybir
+from concourse.masks import make_identity
+
+F32 = mybir.dt.float32
+BF16 = mybir.dt.bfloat16
+I32 = mybir.dt.int32
+U32 = mybir.dt.uint32
+U8 = mybir.dt.uint8
+FP8X4 = mybir.dt.float8_e4m3fn_x4
+ACT = mybir.ActivationFunctionType
+ALU = mybir.AluOpType
+AXIS = mybir.AxisListType
+
+P = 128
+IMAGES = 6
+CHANNELS = 512
+POSITIONS = 1024
+OUT_CHANNELS = 128
+SLOTS = CHANNELS // P
+HALF = 512
+HALVES = POSITIONS // HALF
+BLOCK = 128
+BLOCKS = HALF // BLOCK
+PAIR = 2
+
+FLOPS = 2 * IMAGES * POSITIONS * (2 * CHANNELS) * (2 * OUT_CHANNELS)
+
+
+def tile_fr_pb_t_kernel(
+    tc,
+    x1,
+    x2,
+    FE_x1,
+    FE_x2,
+    g1,
+    g2,
+    p1_w_words,
+    p1_w_scales,
+    p1_b,
+    p2_w_words,
+    p2_w_scales,
+    p2_b,
+    out_0,
+    out_1,
+):
+    nc = tc.nc
+
+    def by_channel(feature_map):
+        return feature_map.rearrange(
+            "n (j0 pp j1 e) h w -> n j0 j1 pp e (h w)", j0=2, pp=P // 2, j1=2, e=2
+        )
+
+    streams = (by_channel(x1), by_channel(x2))
+    extras = (by_channel(FE_x1), by_channel(FE_x2))
+    outs = (
+        out_0.rearrange("n o h w -> n o (h w)"),
+        out_1.rearrange("n o h w -> n o (h w)"),
+    )
+
+    with ExitStack() as ctx:
+        const = ctx.enter_context(tc.tile_pool(name="const", bufs=1))
+        raw_pool = ctx.enter_context(tc.tile_pool(name="raw", bufs=3))
+        wide_pool = ctx.enter_context(tc.tile_pool(name="wide", bufs=2))
+        work = ctx.enter_context(tc.tile_pool(name="work", bufs=3))
+        small = ctx.enter_context(tc.tile_pool(name="small", bufs=4))
+        mx_pool = ctx.enter_context(tc.tile_pool(name="mx", bufs=2))
+        out_pool = ctx.enter_context(tc.tile_pool(name="outp", bufs=4))
+        psum_r = ctx.enter_context(tc.psum_pool(name="psum_r", bufs=3))
+        psum_t = ctx.enter_context(tc.psum_pool(name="psum_t", bufs=2))
+        psum_misc = ctx.enter_context(tc.psum_pool(name="psum_misc", bufs=3))
+
+        ident_f32 = const.tile([P, P], F32)
+        make_identity(nc, ident_f32[:])
+        ident_bf16 = const.tile([P, P], BF16)
+        make_identity(nc, ident_bf16[:])
+
+        gate_rows = const.tile([P, CHANNELS], BF16)
+        nc.vector.memset(gate_rows[:], 0.0)
+        nc.sync.dma_start(out=gate_rows[0:IMAGES, :], in_=g1)
+        nc.sync.dma_start(out=gate_rows[IMAGES : 2 * IMAGES, :], in_=g2)
+        gate_sorted = const.tile([P, SLOTS, P], BF16)
+        rows_view = gate_rows[:].rearrange(
+            "r (j0 pp j1 e) -> r j0 j1 pp e", j0=2, pp=P // 2, j1=2, e=2
+        )
+        for j in range(SLOTS):
+            nc.vector.tensor_copy(
+                out=gate_sorted[:, j, :].rearrange("r (pp e) -> r pp e", e=2),
+                in_=rows_view[:, j % 2, j // 2],
+            )
+        gate_ps = psum_misc.tile([P, SLOTS, P], BF16, tag="misc")
+        for j in range(SLOTS):
+            nc.tensor.transpose(gate_ps[:, j, :], gate_sorted[:, j, :], ident_bf16[:])
+        gates = const.tile([P, SLOTS, P], F32)
+        nc.scalar.activation(out=gates[:], in_=gate_ps[:], func=ACT.Sigmoid)
+
+        bias_rows = const.tile([P, P], BF16)
+        nc.vector.memset(bias_rows[:], 0.0)
+        nc.sync.dma_start(out=bias_rows[0:1, :], in_=p1_b.rearrange("(r o) -> r o", r=1))
+        nc.sync.dma_start(out=bias_rows[1:2, :], in_=p2_b.rearrange("(r o) -> r o", r=1))
+        bias_ps = psum_misc.tile([P, P], BF16, tag="misc")
+        nc.tensor.transpose(bias_ps[:], bias_rows[:], ident_bf16[:])
+        biases = const.tile([P, 2], F32)
+        nc.vector.tensor_copy(out=biases[:], in_=bias_ps[:, 0:2])
+
+        w_words = const.tile([P, 2, 2, OUT_CHANNELS], U32, align_bytes=64)
+        w_scales = const.tile([P, 2, 2, OUT_CHANNELS], U8, align_bytes=64)
+        nc.vector.memset(w_scales[:].bitcast(I32), 0)
+        for w, (words, scales) in enumerate(
+            ((p1_w_words, p1_w_scales), (p2_w_words, p2_w_scales))
+        ):
+            nc.sync.dma_start(
+                out=w_words[:, w].bitcast(I32),
+                in_=words.rearrange("g p n t -> p g (n t)").bitcast(I32),
+            )
+            for quadrant in range(4):
+                nc.sync.dma_start(
+                    out=w_scales[32 * quadrant : 32 * quadrant + 4, w].bitcast(I32),
+                    in_=scales[:, 4 * quadrant : 4 * quadrant + 4, :]
+                    .rearrange("g q n -> q g n")
+                    .bitcast(I32),
+                )
+
+        def load(view, n, h, name):
+            raw = raw_pool.tile([P, SLOTS, HALF], BF16, name=name)
+            for j in range(SLOTS):
+                nc.sync.dma_start(
+                    out=raw[:, j, :],
+                    in_=view[n, j % 2, j // 2, :, :, h * HALF : (h + 1) * HALF],
+                )
+            return raw
+
+        def widen(raw, name):
+            wide = wide_pool.tile([P, SLOTS, HALF], F32, name=name)
+            nc.gpsimd.tensor_scalar(
+                out=wide[:], in0=raw[:], scalar1=1.0, scalar2=0.0, op0=ALU.mult, op1=ALU.add
+            )
+            return wide
+
+        def widen_gated(raw, i, n, name):
+            wide = wide_pool.tile([P, SLOTS, HALF], F32, name=name)
+            column = IMAGES * i + n
+            for j in range(SLOTS):
+                nc.gpsimd.tensor_scalar(
+                    out=wide[:, j, :],
+                    in0=raw[:, j, :],
+                    scalar1=gates[:, j, column : column + 1],
+                    scalar2=0.0,
+                    op0=ALU.mult,
+                    op1=ALU.add,
+                )
+            return wide
+
+        def sum_by_position(bank, first, second, b):
+            columns = slice(b * BLOCK, (b + 1) * BLOCK)
+            for j in range(SLOTS):
+                nc.tensor.matmul(
+                    bank[:, j, :],
+                    lhsT=first[:, j, columns],
+                    rhs=ident_f32[:],
+                    is_transpose=True,
+                    start=True,
+                    stop=False,
+                )
+                nc.tensor.matmul(
+                    bank[:, j, :],
+                    lhsT=second[:, j, columns],
+                    rhs=ident_f32[:],
+                    is_transpose=True,
+                    start=False,
+                    stop=True,
+                )
+
+        def spatial_gate(gated, other):
+            sum_e = small.tile([P, BLOCKS], F32)
+            sum_er = small.tile([P, BLOCKS], F32)
+            for b in range(BLOCKS):
+                r_ps = psum_r.tile([P, SLOTS, P], F32)
+                sum_by_position(r_ps, gated, other, b)
+                r_flat = r_ps[:].rearrange("q j c -> q (j c)")
+                a = work.tile([P, CHANNELS], F32)
+                nc.scalar.activation(out=a[:], in_=r_flat, func=ACT.Exp)
+                a_max = small.tile([P, 1], F32)
+                nc.vector.tensor_reduce(out=a_max[:], in_=a[:], axis=AXIS.X, op=ALU.max)
+                minus_max = small.tile([P, 1], F32)
+                nc.vector.tensor_scalar_mul(out=minus_max[:], in0=a_max[:], scalar1=-1.0)
+                e = work.tile([P, CHANNELS], F32)
+                nc.scalar.activation(
+                    out=e[:],
+                    in_=a[:],
+                    func=ACT.Exp,
+                    bias=minus_max[:, 0:1],
+                    scale=1.0,
+                    accum_out=sum_e[:, b : b + 1],
+                )
+                products = work.tile([P, CHANNELS], BF16)
+                nc.vector.scalar_tensor_tensor(
+                    out=products[:],
+                    in0=e[:],
+                    scalar=1.0,
+                    in1=r_flat,
+                    op0=ALU.mult,
+                    op1=ALU.mult,
+                    accum_out=sum_er[:, b : b + 1],
+                )
+            one_over = small.tile([P, BLOCKS], F32)
+            nc.vector.reciprocal(out=one_over[:], in_=sum_e[:])
+            s = small.tile([P, BLOCKS], F32)
+            nc.vector.tensor_mul(out=s[:], in0=sum_er[:], in1=one_over[:])
+            return s
+
+        def fuse_and_quantise(raw_own, wide_other, wide_extra, s, codes, scales):
+            grouped = mx_pool.tile([P, HALF, SLOTS], BF16, align_bytes=64, bufs=3)
+            grouped_words = (
+                grouped[:]
+                .rearrange("q w t -> q (w t)")
+                .bitcast(F32)
+                .rearrange("q (w u) -> q w u", u=2)
+            )
+            for pair in range(BLOCKS // PAIR):
+                own_ps = psum_misc.tile([P, PAIR, CHANNELS], BF16, tag="misc")
+                for k in range(PAIR):
+                    b = pair * PAIR + k
+                    for j in range(SLOTS):
+                        nc.tensor.transpose(
+                            own_ps[:, k, j * P : (j + 1) * P],
+                            raw_own[:, j, b * BLOCK : (b + 1) * BLOCK],
+                            ident_bf16[:],
+                        )
+                own = work.tile([P, PAIR, CHANNELS], BF16)
+                nc.scalar.copy(out=own[:], in_=own_ps[:])
+                back_ps = psum_misc.tile([P, 2, PAIR * BLOCK], F32, tag="misc")
+                for k in range(PAIR):
+                    b = pair * PAIR + k
+                    t_ps = psum_t.tile([P, SLOTS, P], F32)
+                    sum_by_position(t_ps, wide_other, wide_extra, b)
+                    co = work.tile([P, CHANNELS], BF16, bufs=4)
+                    nc.vector.scalar_tensor_tensor(
+                        out=co[:],
+                        in0=own[:, k, :],
+                        scalar=s[:, b : b + 1],
+                        in1=t_ps[:].rearrange("q j c -> q (j c)"),
+                        op0=ALU.mult,
+                        op1=ALU.add,
+                    )
+                    co_words = co[:].bitcast(F32)
+                    for u in range(2):
+                        nc.tensor.transpose(
+                            back_ps[:, u, k * BLOCK : (k + 1) * BLOCK],
+                            co_words[:, u * P : (u + 1) * P],
+                            ident_f32[:],
+                        )
+                first = pair * PAIR * BLOCK
+                nc.scalar.copy(
+                    out=grouped_words[:, first : first + PAIR * BLOCK, :],
+                    in_=back_ps[:].rearrange("q u w -> q w u"),
+                )
+            nc.vector.quantize_mx(
+                out=codes.bitcast(FP8X4),
+                scales=scales,
+                in_=grouped[:].rearrange("q w t -> q (w t)"),
+            )
+
+        for n in range(IMAGES):
+            for h in range(HALVES):
+                raw_x = [load(streams[i], n, h, "raw_x%d" % i) for i in range(2)]
+                raw_fe = [load(extras[i], n, h, "raw_fe%d" % i) for i in range(2)]
+                gated = [None, None]
+                wide_x = [None, None]
+                for i in range(2):
+                    gated[i] = widen_gated(raw_x[i], i, n, "gated%d" % i)
+                    wide_x[1 - i] = widen(raw_x[1 - i], "wide_x%d" % (1 - i))
+                wide_fe = [widen(raw_fe[i], "wide_fe%d" % i) for i in range(2)]
+
+                re_codes = mx_pool.tile([P, 2, HALF], U32, align_bytes=64)
+                re_scales = mx_pool.tile([P, 2, HALF], U8, align_bytes=64)
+                for i in range(2):
+                    s = spatial_gate(gated[i], wide_x[1 - i])
+                    fuse_and_quantise(
+                        raw_x[i],
+                        wide_x[1 - i],
+                        wide_fe[i],
+                        s,
+                        re_codes[:, i, :],
+                        re_scales[:, i, :],
+                    )
+
+                for w in range(2):
+                    po_ps = psum_misc.tile([P, HALF], F32, tag="misc")
+                    for g in range(2):
+                        nc.tensor.matmul_mx(
+                            out=po_ps[:],
+                            lhsT=w_words[:, w, g, :].bitcast(FP8X4),
+                            lhsT_scale=w_scales[:, w, g, :],
+                            rhs=re_codes[:, g, :].bitcast(FP8X4),
+                            rhs_scale=re_scales[:, g, :],
+                            start=(g == 0),
+                            stop=(g == 1),
+                        )
+                    po = out_pool.tile([P, HALF], F32)
+                    nc.scalar.activation(
+                        out=po[:], in_=po_ps[:], func=ACT.Identity, bias=biases[:, w : w + 1], scale=1.0
+                    )
+                    nc.sync.dma_start(out=outs[w][n, :, h * HALF : (h + 1) * HALF], in_=po[:])

@@ -24,6 +24,9 @@ HALVES = POSITIONS // HALF
 BLOCK = 128
 BLOCKS = HALF // BLOCK
 PAIR = 2
+GROUP = BLOCKS
+UNIT = 2 * GROUP
+JOBS = IMAGES * HALVES * UNIT
 
 FLOPS = 2 * IMAGES * POSITIONS * (2 * CHANNELS) * (2 * OUT_CHANNELS)
 
@@ -69,7 +72,7 @@ def tile_fr_pb_t_kernel(
         out_pool = ctx.enter_context(tc.tile_pool(name="outp", bufs=4))
         psum_r = ctx.enter_context(tc.psum_pool(name="psum_r", bufs=3))
         psum_t = ctx.enter_context(tc.psum_pool(name="psum_t", bufs=2))
-        psum_misc = ctx.enter_context(tc.psum_pool(name="psum_misc", bufs=3))
+        psum_one = ctx.enter_context(tc.psum_pool(name="psum_one", bufs=1))
 
         ident_f32 = const.tile([P, P], F32)
         make_identity(nc, ident_f32[:])
@@ -89,7 +92,7 @@ def tile_fr_pb_t_kernel(
                 out=gate_sorted[:, j, :].rearrange("r (pp e) -> r pp e", e=2),
                 in_=rows_view[:, j % 2, j // 2],
             )
-        gate_ps = psum_misc.tile([P, SLOTS, P], BF16, tag="misc")
+        gate_ps = psum_one.tile([P, SLOTS, P], BF16, tag="own")
         for j in range(SLOTS):
             nc.tensor.transpose(gate_ps[:, j, :], gate_sorted[:, j, :], ident_bf16[:])
         gates = const.tile([P, SLOTS, P], F32)
@@ -99,7 +102,7 @@ def tile_fr_pb_t_kernel(
         nc.vector.memset(bias_rows[:], 0.0)
         nc.sync.dma_start(out=bias_rows[0:1, :], in_=p1_b.rearrange("(r o) -> r o", r=1))
         nc.sync.dma_start(out=bias_rows[1:2, :], in_=p2_b.rearrange("(r o) -> r o", r=1))
-        bias_ps = psum_misc.tile([P, P], BF16, tag="misc")
+        bias_ps = psum_one.tile([P, P], BF16, tag="back")
         nc.tensor.transpose(bias_ps[:], bias_rows[:], ident_bf16[:])
         biases = const.tile([P, 2], F32)
         nc.vector.tensor_copy(out=biases[:], in_=bias_ps[:, 0:2])
@@ -122,35 +125,80 @@ def tile_fr_pb_t_kernel(
                     .bitcast(I32),
                 )
 
-        def load(view, n, h, name):
-            raw = raw_pool.tile([P, SLOTS, HALF], BF16, name=name)
-            for j in range(SLOTS):
-                nc.sync.dma_start(
-                    out=raw[:, j, :],
-                    in_=view[n, j % 2, j // 2, :, :, h * HALF : (h + 1) * HALF],
-                )
-            return raw
+        raw = {}
+        wide = {}
+        r_bank = {}
+        a_tile = {}
+        minus_max = {}
+        e_tile = {}
+        sums = {}
+        s_tile = {}
+        own_bank = {}
+        own_tile = {}
+        t_bank = {}
+        co_tile = {}
+        back_bank = {}
+        grouped_tile = {}
+        re_codes = {}
+        re_scales = {}
+        po_bank = {}
 
-        def widen(raw, name):
-            wide = wide_pool.tile([P, SLOTS, HALF], F32, name=name)
-            nc.gpsimd.tensor_scalar(
-                out=wide[:], in0=raw[:], scalar1=1.0, scalar2=0.0, op0=ALU.mult, op1=ALU.add
-            )
-            return wide
+        def starts(job, size):
+            return 0 <= job < JOBS and job % size == 0
 
-        def widen_gated(raw, i, n, name):
-            wide = wide_pool.tile([P, SLOTS, HALF], F32, name=name)
-            column = IMAGES * i + n
-            for j in range(SLOTS):
+        def place(job):
+            group, b = divmod(job, GROUP)
+            unit, i = divmod(group, 2)
+            return unit, i, b
+
+        def load_unit(job):
+            if not starts(job, UNIT):
+                return
+            unit = job // UNIT
+            n, h = divmod(unit, HALVES)
+            for name, view in (
+                ("x0", streams[0]),
+                ("x1", streams[1]),
+                ("fe0", extras[0]),
+                ("fe1", extras[1]),
+            ):
+                tile = raw_pool.tile([P, SLOTS, HALF], BF16, name="raw_" + name)
+                for j in range(SLOTS):
+                    nc.sync.dma_start(
+                        out=tile[:, j, :],
+                        in_=view[n, j % 2, j // 2, :, :, h * HALF : (h + 1) * HALF],
+                    )
+                raw[unit, name] = tile
+
+        def widen_group(job):
+            if not starts(job, GROUP):
+                return
+            unit, i, b = place(job)
+            n = unit // HALVES
+            for kind, name in (("other", "x%d" % (1 - i)), ("extra", "fe%d" % i)):
+                tile = wide_pool.tile([P, SLOTS, HALF], F32, name="wide_%s%d" % (kind, i))
                 nc.gpsimd.tensor_scalar(
-                    out=wide[:, j, :],
-                    in0=raw[:, j, :],
-                    scalar1=gates[:, j, column : column + 1],
+                    out=tile[:],
+                    in0=raw[unit, name][:],
+                    scalar1=1.0,
                     scalar2=0.0,
                     op0=ALU.mult,
                     op1=ALU.add,
                 )
-            return wide
+                wide[unit, i, kind] = tile
+                if kind == "other":
+                    gated = wide_pool.tile([P, SLOTS, HALF], F32, name="wide_gated%d" % i)
+                    column = IMAGES * i + n
+                    for j in range(SLOTS):
+                        nc.gpsimd.tensor_scalar(
+                            out=gated[:, j, :],
+                            in0=raw[unit, "x%d" % i][:, j, :],
+                            scalar1=gates[:, j, column : column + 1],
+                            scalar2=0.0,
+                            op0=ALU.mult,
+                            op1=ALU.add,
+                        )
+                    wide[unit, i, "gated"] = gated
 
         def sum_by_position(bank, first, second, b):
             columns = slice(b * BLOCK, (b + 1) * BLOCK)
@@ -172,134 +220,203 @@ def tile_fr_pb_t_kernel(
                     stop=True,
                 )
 
-        def spatial_gate(gated, other):
-            sum_e = small.tile([P, BLOCKS], F32)
-            sum_er = small.tile([P, BLOCKS], F32)
-            for b in range(BLOCKS):
-                r_ps = psum_r.tile([P, SLOTS, P], F32)
-                sum_by_position(r_ps, gated, other, b)
-                r_flat = r_ps[:].rearrange("q j c -> q (j c)")
-                a = work.tile([P, CHANNELS], F32)
-                nc.scalar.activation(out=a[:], in_=r_flat, func=ACT.Exp)
-                a_max = small.tile([P, 1], F32)
-                nc.vector.tensor_reduce(out=a_max[:], in_=a[:], axis=AXIS.X, op=ALU.max)
-                minus_max = small.tile([P, 1], F32)
-                nc.vector.tensor_scalar_mul(out=minus_max[:], in0=a_max[:], scalar1=-1.0)
-                e = work.tile([P, CHANNELS], F32)
-                nc.scalar.activation(
-                    out=e[:],
-                    in_=a[:],
-                    func=ACT.Exp,
-                    bias=minus_max[:, 0:1],
-                    scale=1.0,
-                    accum_out=sum_e[:, b : b + 1],
-                )
-                products = work.tile([P, CHANNELS], BF16)
-                nc.vector.scalar_tensor_tensor(
-                    out=products[:],
-                    in0=e[:],
-                    scalar=1.0,
-                    in1=r_flat,
-                    op0=ALU.mult,
-                    op1=ALU.mult,
-                    accum_out=sum_er[:, b : b + 1],
-                )
-            one_over = small.tile([P, BLOCKS], F32)
-            nc.vector.reciprocal(out=one_over[:], in_=sum_e[:])
-            s = small.tile([P, BLOCKS], F32)
-            nc.vector.tensor_mul(out=s[:], in0=sum_er[:], in1=one_over[:])
-            return s
+        def sum_r(job):
+            if not starts(job, 1):
+                return
+            unit, i, b = place(job)
+            bank = psum_r.tile([P, SLOTS, P], F32, name="r_ps")
+            sum_by_position(bank, wide[unit, i, "gated"], wide[unit, i, "other"], b)
+            r_bank[job] = bank[:].rearrange("q j c -> q (j c)")
 
-        def fuse_and_quantise(raw_own, wide_other, wide_extra, s, codes, scales):
-            grouped = mx_pool.tile([P, HALF, SLOTS], BF16, align_bytes=64, bufs=3)
+        def exp_a(job):
+            if not starts(job, 1):
+                return
+            a_tile[job] = work.tile([P, CHANNELS], F32, name="a")
+            nc.scalar.activation(out=a_tile[job][:], in_=r_bank[job], func=ACT.Exp)
+
+        def find_max(job):
+            if not starts(job, 1):
+                return
+            minus_max[job] = small.tile([P, 1], F32, name="minus_max")
+            nc.vector.tensor_reduce(
+                out=minus_max[job][:], in_=a_tile[job][:], axis=AXIS.X, op=ALU.max, negate=True
+            )
+
+        def exp_e(job):
+            if not starts(job, 1):
+                return
+            group, b = divmod(job, GROUP)
+            if b == 0:
+                sums[group, "e"] = small.tile([P, GROUP], F32, name="sum_e")
+            e_tile[job] = work.tile([P, CHANNELS], F32, name="e")
+            nc.scalar.activation(
+                out=e_tile[job][:],
+                in_=a_tile[job][:],
+                func=ACT.Exp,
+                bias=minus_max[job][:, 0:1],
+                scale=1.0,
+                accum_out=sums[group, "e"][:, b : b + 1],
+            )
+
+        def sum_er(job):
+            if not starts(job, 1):
+                return
+            group, b = divmod(job, GROUP)
+            if b == 0:
+                sums[group, "er"] = small.tile([P, GROUP], F32, name="sum_er")
+            products = work.tile([P, CHANNELS], BF16, name="products")
+            nc.vector.scalar_tensor_tensor(
+                out=products[:],
+                in0=e_tile[job][:],
+                scalar=1.0,
+                in1=r_bank[job],
+                op0=ALU.mult,
+                op1=ALU.mult,
+                accum_out=sums[group, "er"][:, b : b + 1],
+            )
+            if b == GROUP - 1:
+                one_over = small.tile([P, GROUP], F32, name="one_over")
+                nc.vector.reciprocal(out=one_over[:], in_=sums[group, "e"][:])
+                s_tile[group] = small.tile([P, GROUP], F32, name="s")
+                nc.vector.tensor_mul(
+                    out=s_tile[group][:], in0=sums[group, "er"][:], in1=one_over[:]
+                )
+
+        def own_transposes(job):
+            if not starts(job, PAIR):
+                return
+            unit, i, b = place(job)
+            own_bank[job] = psum_one.tile([P, PAIR, CHANNELS], BF16, name="own_ps", tag="own")
+            for k in range(PAIR):
+                for j in range(SLOTS):
+                    nc.tensor.transpose(
+                        own_bank[job][:, k, j * P : (j + 1) * P],
+                        raw[unit, "x%d" % i][:, j, (b + k) * BLOCK : (b + k + 1) * BLOCK],
+                        ident_bf16[:],
+                    )
+
+        def own_copy(job):
+            if not starts(job, PAIR):
+                return
+            own_tile[job] = work.tile([P, PAIR, CHANNELS], BF16, name="own")
+            nc.scalar.copy(out=own_tile[job][:], in_=own_bank[job][:])
+
+        def sum_t(job):
+            if not starts(job, 1):
+                return
+            unit, i, b = place(job)
+            bank = psum_t.tile([P, SLOTS, P], F32, name="t_ps")
+            sum_by_position(bank, wide[unit, i, "other"], wide[unit, i, "extra"], b)
+            t_bank[job] = bank[:].rearrange("q j c -> q (j c)")
+
+        def fuse(job):
+            if not starts(job, 1):
+                return
+            group, b = divmod(job, GROUP)
+            co_tile[job] = work.tile([P, CHANNELS], BF16, name="co")
+            nc.vector.scalar_tensor_tensor(
+                out=co_tile[job][:],
+                in0=own_tile[job - job % PAIR][:, job % PAIR, :],
+                scalar=s_tile[group][:, b : b + 1],
+                in1=t_bank[job],
+                op0=ALU.mult,
+                op1=ALU.add,
+            )
+
+        def back_transposes(job):
+            if not starts(job, 1):
+                return
+            k = job % PAIR
+            if k == 0:
+                back_bank[job] = psum_one.tile([P, 2, PAIR * BLOCK], F32, name="back_ps", tag="back")
+            co_words = co_tile[job][:].bitcast(F32)
+            for u in range(2):
+                nc.tensor.transpose(
+                    back_bank[job - k][:, u, k * BLOCK : (k + 1) * BLOCK],
+                    co_words[:, u * P : (u + 1) * P],
+                    ident_f32[:],
+                )
+
+        def back_copy(job):
+            if not starts(job, PAIR):
+                return
+            group, b = divmod(job, GROUP)
+            if b == 0:
+                grouped_tile[group] = mx_pool.tile(
+                    [P, HALF, SLOTS], BF16, name="grouped", align_bytes=64
+                )
             grouped_words = (
-                grouped[:]
+                grouped_tile[group][:]
                 .rearrange("q w t -> q (w t)")
                 .bitcast(F32)
                 .rearrange("q (w u) -> q w u", u=2)
             )
-            for pair in range(BLOCKS // PAIR):
-                own_ps = psum_misc.tile([P, PAIR, CHANNELS], BF16, tag="misc")
-                for k in range(PAIR):
-                    b = pair * PAIR + k
-                    for j in range(SLOTS):
-                        nc.tensor.transpose(
-                            own_ps[:, k, j * P : (j + 1) * P],
-                            raw_own[:, j, b * BLOCK : (b + 1) * BLOCK],
-                            ident_bf16[:],
-                        )
-                own = work.tile([P, PAIR, CHANNELS], BF16)
-                nc.scalar.copy(out=own[:], in_=own_ps[:])
-                back_ps = psum_misc.tile([P, 2, PAIR * BLOCK], F32, tag="misc")
-                for k in range(PAIR):
-                    b = pair * PAIR + k
-                    t_ps = psum_t.tile([P, SLOTS, P], F32)
-                    sum_by_position(t_ps, wide_other, wide_extra, b)
-                    co = work.tile([P, CHANNELS], BF16, bufs=4)
-                    nc.vector.scalar_tensor_tensor(
-                        out=co[:],
-                        in0=own[:, k, :],
-                        scalar=s[:, b : b + 1],
-                        in1=t_ps[:].rearrange("q j c -> q (j c)"),
-                        op0=ALU.mult,
-                        op1=ALU.add,
-                    )
-                    co_words = co[:].bitcast(F32)
-                    for u in range(2):
-                        nc.tensor.transpose(
-                            back_ps[:, u, k * BLOCK : (k + 1) * BLOCK],
-                            co_words[:, u * P : (u + 1) * P],
-                            ident_f32[:],
-                        )
-                first = pair * PAIR * BLOCK
-                nc.scalar.copy(
-                    out=grouped_words[:, first : first + PAIR * BLOCK, :],
-                    in_=back_ps[:].rearrange("q u w -> q w u"),
-                )
-            nc.vector.quantize_mx(
-                out=codes.bitcast(FP8X4),
-                scales=scales,
-                in_=grouped[:].rearrange("q w t -> q (w t)"),
+            nc.scalar.copy(
+                out=grouped_words[:, b * BLOCK : (b + PAIR) * BLOCK, :],
+                in_=back_bank[job][:].rearrange("q u w -> q w u"),
             )
 
-        for n in range(IMAGES):
-            for h in range(HALVES):
-                raw_x = [load(streams[i], n, h, "raw_x%d" % i) for i in range(2)]
-                raw_fe = [load(extras[i], n, h, "raw_fe%d" % i) for i in range(2)]
-                gated = [None, None]
-                wide_x = [None, None]
-                for i in range(2):
-                    gated[i] = widen_gated(raw_x[i], i, n, "gated%d" % i)
-                    wide_x[1 - i] = widen(raw_x[1 - i], "wide_x%d" % (1 - i))
-                wide_fe = [widen(raw_fe[i], "wide_fe%d" % i) for i in range(2)]
+        def quantise(job):
+            if not starts(job, GROUP):
+                return
+            unit, i, b = place(job)
+            if i == 0:
+                re_codes[unit] = mx_pool.tile([P, 2, HALF], U32, name="re_codes", align_bytes=64)
+                re_scales[unit] = mx_pool.tile([P, 2, HALF], U8, name="re_scales", align_bytes=64)
+            nc.vector.quantize_mx(
+                out=re_codes[unit][:, i, :].bitcast(FP8X4),
+                scales=re_scales[unit][:, i, :],
+                in_=grouped_tile[job // GROUP][:].rearrange("q w t -> q (w t)"),
+            )
 
-                re_codes = mx_pool.tile([P, 2, HALF], U32, align_bytes=64)
-                re_scales = mx_pool.tile([P, 2, HALF], U8, align_bytes=64)
-                for i in range(2):
-                    s = spatial_gate(gated[i], wide_x[1 - i])
-                    fuse_and_quantise(
-                        raw_x[i],
-                        wide_x[1 - i],
-                        wide_fe[i],
-                        s,
-                        re_codes[:, i, :],
-                        re_scales[:, i, :],
-                    )
+        def project(job, w):
+            if not starts(job, UNIT):
+                return
+            unit = job // UNIT
+            po_bank[unit, w] = psum_one.tile([P, HALF], F32, name="po_ps", tag="po")
+            for g in range(2):
+                nc.tensor.matmul_mx(
+                    out=po_bank[unit, w][:],
+                    lhsT=w_words[:, w, g, :].bitcast(FP8X4),
+                    lhsT_scale=w_scales[:, w, g, :],
+                    rhs=re_codes[unit][:, g, :].bitcast(FP8X4),
+                    rhs_scale=re_scales[unit][:, g, :],
+                    start=(g == 0),
+                    stop=(g == 1),
+                )
 
-                for w in range(2):
-                    po_ps = psum_misc.tile([P, HALF], F32, tag="misc")
-                    for g in range(2):
-                        nc.tensor.matmul_mx(
-                            out=po_ps[:],
-                            lhsT=w_words[:, w, g, :].bitcast(FP8X4),
-                            lhsT_scale=w_scales[:, w, g, :],
-                            rhs=re_codes[:, g, :].bitcast(FP8X4),
-                            rhs_scale=re_scales[:, g, :],
-                            start=(g == 0),
-                            stop=(g == 1),
-                        )
-                    po = out_pool.tile([P, HALF], F32)
-                    nc.scalar.activation(
-                        out=po[:], in_=po_ps[:], func=ACT.Identity, bias=biases[:, w : w + 1], scale=1.0
-                    )
-                    nc.sync.dma_start(out=outs[w][n, :, h * HALF : (h + 1) * HALF], in_=po[:])
+        def add_bias_and_store(job, w):
+            if not starts(job, UNIT):
+                return
+            unit = job // UNIT
+            n, h = divmod(unit, HALVES)
+            po = out_pool.tile([P, HALF], F32, name="po")
+            nc.scalar.activation(
+                out=po[:],
+                in_=po_bank[unit, w][:],
+                func=ACT.Identity,
+                bias=biases[:, w : w + 1],
+                scale=1.0,
+            )
+            nc.sync.dma_start(out=outs[w][n, :, h * HALF : (h + 1) * HALF], in_=po[:])
+
+        with tc.manual_schedule():
+            for t in range(-12, JOBS + 19):
+                load_unit(t + 12)
+                widen_group(t + 8)
+                fuse(t - 5)
+                sum_r(t + 1)
+                exp_a(t)
+                exp_e(t - 1)
+                find_max(t)
+                sum_er(t - 1)
+                sum_t(t - 4)
+                own_transposes(t - 3)
+                own_copy(t - 4)
+                back_copy(t - 7)
+                back_transposes(t - 5)
+                quantise(t - 10)
+                project(t - 15, 0)
+                add_bias_and_store(t - 16, 0)
+                project(t - 17, 1)
+                add_bias_and_store(t - 18, 1)

@@ -22,9 +22,8 @@ SLOTS = CHANNELS // P
 HALF = 512
 HALVES = POSITIONS // HALF
 BLOCK = 128
-BLOCKS = HALF // BLOCK
 PAIR = 2
-GROUP = BLOCKS
+GROUP = HALF // BLOCK
 UNIT = 2 * GROUP
 JOBS = IMAGES * HALVES * UNIT
 
@@ -51,9 +50,7 @@ def tile_fr_pb_t_kernel(
     nc = tc.nc
 
     def by_channel(feature_map):
-        return feature_map.rearrange(
-            "n (j0 pp j1 e) h w -> n j0 j1 pp e (h w)", j0=2, pp=P // 2, j1=2, e=2
-        )
+        return feature_map.rearrange("n (p j) h w -> n p j (h w)", j=SLOTS)
 
     streams = (by_channel(x1), by_channel(x2))
     extras = (by_channel(FE_x1), by_channel(FE_x2))
@@ -65,14 +62,15 @@ def tile_fr_pb_t_kernel(
     with ExitStack() as ctx:
         const = ctx.enter_context(tc.tile_pool(name="const", bufs=1))
         raw_pool = ctx.enter_context(tc.tile_pool(name="raw", bufs=3))
-        wide_pool = ctx.enter_context(tc.tile_pool(name="wide", bufs=2))
+        wide_pool = ctx.enter_context(tc.tile_pool(name="wide", bufs=3))
         work = ctx.enter_context(tc.tile_pool(name="work", bufs=3))
         small = ctx.enter_context(tc.tile_pool(name="small", bufs=4))
         mx_pool = ctx.enter_context(tc.tile_pool(name="mx", bufs=2))
         out_pool = ctx.enter_context(tc.tile_pool(name="outp", bufs=4))
         psum_r = ctx.enter_context(tc.psum_pool(name="psum_r", bufs=3))
-        psum_t = ctx.enter_context(tc.psum_pool(name="psum_t", bufs=2))
-        psum_one = ctx.enter_context(tc.psum_pool(name="psum_one", bufs=1))
+        psum_own = ctx.enter_context(tc.psum_pool(name="psum_own", bufs=2))
+        psum_u = ctx.enter_context(tc.psum_pool(name="psum_u", bufs=2))
+        psum_po = ctx.enter_context(tc.psum_pool(name="psum_po", bufs=1))
 
         ident_f32 = const.tile([P, P], F32)
         make_identity(nc, ident_f32[:])
@@ -84,15 +82,10 @@ def tile_fr_pb_t_kernel(
         nc.sync.dma_start(out=gate_rows[0:IMAGES, :], in_=g1)
         nc.sync.dma_start(out=gate_rows[IMAGES : 2 * IMAGES, :], in_=g2)
         gate_sorted = const.tile([P, SLOTS, P], BF16)
-        rows_view = gate_rows[:].rearrange(
-            "r (j0 pp j1 e) -> r j0 j1 pp e", j0=2, pp=P // 2, j1=2, e=2
+        nc.vector.tensor_copy(
+            out=gate_sorted[:], in_=gate_rows[:].rearrange("r (p j) -> r j p", j=SLOTS)
         )
-        for j in range(SLOTS):
-            nc.vector.tensor_copy(
-                out=gate_sorted[:, j, :].rearrange("r (pp e) -> r pp e", e=2),
-                in_=rows_view[:, j % 2, j // 2],
-            )
-        gate_ps = psum_one.tile([P, SLOTS, P], BF16, tag="own")
+        gate_ps = psum_own.tile([P, SLOTS, P], BF16, tag="own_ps")
         for j in range(SLOTS):
             nc.tensor.transpose(gate_ps[:, j, :], gate_sorted[:, j, :], ident_bf16[:])
         gates = const.tile([P, SLOTS, P], F32)
@@ -102,7 +95,7 @@ def tile_fr_pb_t_kernel(
         nc.vector.memset(bias_rows[:], 0.0)
         nc.sync.dma_start(out=bias_rows[0:1, :], in_=p1_b.rearrange("(r o) -> r o", r=1))
         nc.sync.dma_start(out=bias_rows[1:2, :], in_=p2_b.rearrange("(r o) -> r o", r=1))
-        bias_ps = psum_one.tile([P, P], BF16, tag="back")
+        bias_ps = psum_own.tile([P, P], BF16, tag="own_ps")
         nc.tensor.transpose(bias_ps[:], bias_rows[:], ident_bf16[:])
         biases = const.tile([P, 2], F32)
         nc.vector.tensor_copy(out=biases[:], in_=bias_ps[:, 0:2])
@@ -126,7 +119,9 @@ def tile_fr_pb_t_kernel(
                 )
 
         raw = {}
-        wide = {}
+        gated_tile = {}
+        other_tile = {}
+        rest_tile = {}
         r_bank = {}
         a_tile = {}
         minus_max = {}
@@ -134,10 +129,8 @@ def tile_fr_pb_t_kernel(
         sums = {}
         s_tile = {}
         own_bank = {}
-        own_tile = {}
-        t_bank = {}
-        co_tile = {}
-        back_bank = {}
+        scaled_tile = {}
+        u_bank = {}
         grouped_tile = {}
         re_codes = {}
         re_scales = {}
@@ -162,50 +155,56 @@ def tile_fr_pb_t_kernel(
                 ("fe0", extras[0]),
                 ("fe1", extras[1]),
             ):
-                tile = raw_pool.tile([P, SLOTS, HALF], BF16, name="raw_" + name)
-                for j in range(SLOTS):
-                    nc.sync.dma_start(
-                        out=tile[:, j, :],
-                        in_=view[n, j % 2, j // 2, :, :, h * HALF : (h + 1) * HALF],
-                    )
-                raw[unit, name] = tile
+                raw[unit, name] = raw_pool.tile([P, SLOTS, HALF], BF16, name="raw_" + name)
+                nc.sync.dma_start(
+                    out=raw[unit, name][:], in_=view[n, :, :, h * HALF : (h + 1) * HALF]
+                )
 
-        def widen_group(job):
+        def gate_own(job):
             if not starts(job, GROUP):
                 return
             unit, i, b = place(job)
-            n = unit // HALVES
-            for kind, name in (("other", "x%d" % (1 - i)), ("extra", "fe%d" % i)):
-                tile = wide_pool.tile([P, SLOTS, HALF], F32, name="wide_%s%d" % (kind, i))
+            column = IMAGES * i + unit // HALVES
+            gated_tile[job] = wide_pool.tile([P, SLOTS, HALF], F32, name="gated")
+            for j in range(SLOTS):
                 nc.gpsimd.tensor_scalar(
-                    out=tile[:],
-                    in0=raw[unit, name][:],
-                    scalar1=1.0,
+                    out=gated_tile[job][:, j, :],
+                    in0=raw[unit, "x%d" % i][:, j, :],
+                    scalar1=gates[:, j, column : column + 1],
                     scalar2=0.0,
                     op0=ALU.mult,
                     op1=ALU.add,
                 )
-                wide[unit, i, kind] = tile
-                if kind == "other":
-                    gated = wide_pool.tile([P, SLOTS, HALF], F32, name="wide_gated%d" % i)
-                    column = IMAGES * i + n
-                    for j in range(SLOTS):
-                        nc.gpsimd.tensor_scalar(
-                            out=gated[:, j, :],
-                            in0=raw[unit, "x%d" % i][:, j, :],
-                            scalar1=gates[:, j, column : column + 1],
-                            scalar2=0.0,
-                            op0=ALU.mult,
-                            op1=ALU.add,
-                        )
-                    wide[unit, i, "gated"] = gated
 
-        def sum_by_position(bank, first, second, b):
+        def widen_other(job):
+            if not starts(job, GROUP):
+                return
+            unit, i, b = place(job)
+            other_tile[job] = wide_pool.tile([P, SLOTS, HALF], F32, name="other")
+            nc.vector.tensor_copy(out=other_tile[job][:], in_=raw[unit, "x%d" % (1 - i)][:])
+
+        def add_rest(job):
+            if not starts(job, GROUP):
+                return
+            unit, i, b = place(job)
+            rest_tile[job] = wide_pool.tile([P, SLOTS, HALF], F32, name="rest")
+            nc.gpsimd.tensor_tensor(
+                out=rest_tile[job][:],
+                in0=raw[unit, "x%d" % (1 - i)][:],
+                in1=raw[unit, "fe%d" % i][:],
+                op=ALU.add,
+            )
+
+        def sum_r(job):
+            if not starts(job, 1):
+                return
+            b = job % GROUP
             columns = slice(b * BLOCK, (b + 1) * BLOCK)
+            bank = psum_r.tile([P, SLOTS, P], F32, name="r_ps")
             for j in range(SLOTS):
                 nc.tensor.matmul(
                     bank[:, j, :],
-                    lhsT=first[:, j, columns],
+                    lhsT=gated_tile[job - b][:, j, columns],
                     rhs=ident_f32[:],
                     is_transpose=True,
                     start=True,
@@ -213,19 +212,12 @@ def tile_fr_pb_t_kernel(
                 )
                 nc.tensor.matmul(
                     bank[:, j, :],
-                    lhsT=second[:, j, columns],
+                    lhsT=other_tile[job - b][:, j, columns],
                     rhs=ident_f32[:],
                     is_transpose=True,
                     start=False,
                     stop=True,
                 )
-
-        def sum_r(job):
-            if not starts(job, 1):
-                return
-            unit, i, b = place(job)
-            bank = psum_r.tile([P, SLOTS, P], F32, name="r_ps")
-            sum_by_position(bank, wide[unit, i, "gated"], wide[unit, i, "other"], b)
             r_bank[job] = bank[:].rearrange("q j c -> q (j c)")
 
         def exp_a(job):
@@ -286,7 +278,7 @@ def tile_fr_pb_t_kernel(
             if not starts(job, PAIR):
                 return
             unit, i, b = place(job)
-            own_bank[job] = psum_one.tile([P, PAIR, CHANNELS], BF16, name="own_ps", tag="own")
+            own_bank[job] = psum_own.tile([P, PAIR, CHANNELS], BF16, name="own_ps")
             for k in range(PAIR):
                 for j in range(SLOTS):
                     nc.tensor.transpose(
@@ -295,65 +287,39 @@ def tile_fr_pb_t_kernel(
                         ident_bf16[:],
                     )
 
-        def own_copy(job):
-            if not starts(job, PAIR):
-                return
-            own_tile[job] = work.tile([P, PAIR, CHANNELS], BF16, name="own")
-            nc.scalar.copy(out=own_tile[job][:], in_=own_bank[job][:])
-
-        def sum_t(job):
-            if not starts(job, 1):
-                return
-            unit, i, b = place(job)
-            bank = psum_t.tile([P, SLOTS, P], F32, name="t_ps")
-            sum_by_position(bank, wide[unit, i, "other"], wide[unit, i, "extra"], b)
-            t_bank[job] = bank[:].rearrange("q j c -> q (j c)")
-
-        def fuse(job):
+        def scale_own(job):
             if not starts(job, 1):
                 return
             group, b = divmod(job, GROUP)
-            co_tile[job] = work.tile([P, CHANNELS], BF16, name="co")
-            nc.vector.scalar_tensor_tensor(
-                out=co_tile[job][:],
-                in0=own_tile[job - job % PAIR][:, job % PAIR, :],
-                scalar=s_tile[group][:, b : b + 1],
-                in1=t_bank[job],
-                op0=ALU.mult,
-                op1=ALU.add,
+            scaled_tile[job] = work.tile([P, SLOTS, P], F32, name="scaled")
+            nc.scalar.activation(
+                out=scaled_tile[job][:].rearrange("q j c -> q (j c)"),
+                in_=own_bank[job - job % PAIR][:, job % PAIR, :],
+                func=ACT.Copy,
+                scale=s_tile[group][:, b : b + 1],
             )
 
-        def back_transposes(job):
+        def turn_back(job):
             if not starts(job, 1):
                 return
-            k = job % PAIR
-            if k == 0:
-                back_bank[job] = psum_one.tile([P, 2, PAIR * BLOCK], F32, name="back_ps", tag="back")
-            co_words = co_tile[job][:].bitcast(F32)
-            for u in range(2):
-                nc.tensor.transpose(
-                    back_bank[job - k][:, u, k * BLOCK : (k + 1) * BLOCK],
-                    co_words[:, u * P : (u + 1) * P],
-                    ident_f32[:],
-                )
+            u_bank[job] = psum_u.tile([P, SLOTS, BLOCK], F32, name="u_ps")
+            for j in range(SLOTS):
+                nc.tensor.transpose(u_bank[job][:, j, :], scaled_tile[job][:, j, :], ident_f32[:])
 
-        def back_copy(job):
-            if not starts(job, PAIR):
+        def fuse(job):
+            if not starts(job, 1):
                 return
             group, b = divmod(job, GROUP)
             if b == 0:
                 grouped_tile[group] = mx_pool.tile(
                     [P, HALF, SLOTS], BF16, name="grouped", align_bytes=64
                 )
-            grouped_words = (
-                grouped_tile[group][:]
-                .rearrange("q w t -> q (w t)")
-                .bitcast(F32)
-                .rearrange("q (w u) -> q w u", u=2)
-            )
-            nc.scalar.copy(
-                out=grouped_words[:, b * BLOCK : (b + PAIR) * BLOCK, :],
-                in_=back_bank[job][:].rearrange("q u w -> q w u"),
+            columns = slice(b * BLOCK, (b + 1) * BLOCK)
+            nc.vector.tensor_tensor(
+                out=grouped_tile[group][:, columns, :],
+                in0=u_bank[job][:].rearrange("p j w -> p w j"),
+                in1=rest_tile[job - b][:, :, columns].rearrange("p j w -> p w j"),
+                op=ALU.add,
             )
 
         def quantise(job):
@@ -366,14 +332,14 @@ def tile_fr_pb_t_kernel(
             nc.vector.quantize_mx(
                 out=re_codes[unit][:, i, :].bitcast(FP8X4),
                 scales=re_scales[unit][:, i, :],
-                in_=grouped_tile[job // GROUP][:].rearrange("q w t -> q (w t)"),
+                in_=grouped_tile[job // GROUP][:].rearrange("p w j -> p (w j)"),
             )
 
         def project(job, w):
             if not starts(job, UNIT):
                 return
             unit = job // UNIT
-            po_bank[unit, w] = psum_one.tile([P, HALF], F32, name="po_ps", tag="po")
+            po_bank[unit, w] = psum_po.tile([P, HALF], F32, name="po_ps")
             for g in range(2):
                 nc.tensor.matmul_mx(
                     out=po_bank[unit, w][:],
@@ -403,19 +369,19 @@ def tile_fr_pb_t_kernel(
         with tc.manual_schedule():
             for t in range(-12, JOBS + 19):
                 load_unit(t + 12)
-                widen_group(t + 8)
-                fuse(t - 5)
+                gate_own(t + 8)
+                add_rest(t + 1)
+                fuse(t - 7)
                 sum_r(t + 1)
                 exp_a(t)
                 exp_e(t - 1)
                 find_max(t)
                 sum_er(t - 1)
-                sum_t(t - 4)
-                own_transposes(t - 3)
-                own_copy(t - 4)
-                back_copy(t - 7)
-                back_transposes(t - 5)
+                scale_own(t - 5)
+                turn_back(t - 6)
+                own_transposes(t - 4)
                 quantise(t - 10)
+                widen_other(t + 5)
                 project(t - 15, 0)
                 add_bias_and_store(t - 16, 0)
                 project(t - 17, 1)

@@ -22,8 +22,9 @@ SLOTS = CHANNELS // P
 HALF = 512
 HALVES = POSITIONS // HALF
 BLOCK = 128
+BLOCKS = HALF // BLOCK
 PAIR = 2
-GROUP = HALF // BLOCK
+GROUP = BLOCKS
 UNIT = 2 * GROUP
 JOBS = IMAGES * HALVES * UNIT
 
@@ -50,7 +51,9 @@ def tile_fr_pb_t_kernel(
     nc = tc.nc
 
     def by_channel(feature_map):
-        return feature_map.rearrange("n (p j) h w -> n p j (h w)", j=SLOTS)
+        return feature_map.rearrange(
+            "n (j0 pp j1 e) h w -> n j0 j1 pp e (h w)", j0=2, pp=P // 2, j1=2, e=2
+        )
 
     streams = (by_channel(x1), by_channel(x2))
     extras = (by_channel(FE_x1), by_channel(FE_x2))
@@ -62,15 +65,14 @@ def tile_fr_pb_t_kernel(
     with ExitStack() as ctx:
         const = ctx.enter_context(tc.tile_pool(name="const", bufs=1))
         raw_pool = ctx.enter_context(tc.tile_pool(name="raw", bufs=3))
-        wide_pool = ctx.enter_context(tc.tile_pool(name="wide", bufs=3))
+        wide_pool = ctx.enter_context(tc.tile_pool(name="wide", bufs=2))
         work = ctx.enter_context(tc.tile_pool(name="work", bufs=3))
         small = ctx.enter_context(tc.tile_pool(name="small", bufs=4))
         mx_pool = ctx.enter_context(tc.tile_pool(name="mx", bufs=2))
         out_pool = ctx.enter_context(tc.tile_pool(name="outp", bufs=4))
         psum_r = ctx.enter_context(tc.psum_pool(name="psum_r", bufs=3))
-        psum_own = ctx.enter_context(tc.psum_pool(name="psum_own", bufs=2))
-        psum_u = ctx.enter_context(tc.psum_pool(name="psum_u", bufs=2))
-        psum_po = ctx.enter_context(tc.psum_pool(name="psum_po", bufs=1))
+        psum_t = ctx.enter_context(tc.psum_pool(name="psum_t", bufs=2))
+        psum_one = ctx.enter_context(tc.psum_pool(name="psum_one", bufs=1))
 
         ident_f32 = const.tile([P, P], F32)
         make_identity(nc, ident_f32[:])
@@ -82,10 +84,15 @@ def tile_fr_pb_t_kernel(
         nc.sync.dma_start(out=gate_rows[0:IMAGES, :], in_=g1)
         nc.sync.dma_start(out=gate_rows[IMAGES : 2 * IMAGES, :], in_=g2)
         gate_sorted = const.tile([P, SLOTS, P], BF16)
-        nc.vector.tensor_copy(
-            out=gate_sorted[:], in_=gate_rows[:].rearrange("r (p j) -> r j p", j=SLOTS)
+        rows_view = gate_rows[:].rearrange(
+            "r (j0 pp j1 e) -> r j0 j1 pp e", j0=2, pp=P // 2, j1=2, e=2
         )
-        gate_ps = psum_own.tile([P, SLOTS, P], BF16, tag="own_ps")
+        for j in range(SLOTS):
+            nc.vector.tensor_copy(
+                out=gate_sorted[:, j, :].rearrange("r (pp e) -> r pp e", e=2),
+                in_=rows_view[:, j % 2, j // 2],
+            )
+        gate_ps = psum_one.tile([P, SLOTS, P], BF16, tag="own")
         for j in range(SLOTS):
             nc.tensor.transpose(gate_ps[:, j, :], gate_sorted[:, j, :], ident_bf16[:])
         gates = const.tile([P, SLOTS, P], F32)
@@ -95,7 +102,7 @@ def tile_fr_pb_t_kernel(
         nc.vector.memset(bias_rows[:], 0.0)
         nc.sync.dma_start(out=bias_rows[0:1, :], in_=p1_b.rearrange("(r o) -> r o", r=1))
         nc.sync.dma_start(out=bias_rows[1:2, :], in_=p2_b.rearrange("(r o) -> r o", r=1))
-        bias_ps = psum_own.tile([P, P], BF16, tag="own_ps")
+        bias_ps = psum_one.tile([P, P], BF16, tag="back")
         nc.tensor.transpose(bias_ps[:], bias_rows[:], ident_bf16[:])
         biases = const.tile([P, 2], F32)
         nc.vector.tensor_copy(out=biases[:], in_=bias_ps[:, 0:2])
@@ -119,9 +126,7 @@ def tile_fr_pb_t_kernel(
                 )
 
         raw = {}
-        gated_tile = {}
-        other_tile = {}
-        rest_tile = {}
+        wide = {}
         r_bank = {}
         a_tile = {}
         minus_max = {}
@@ -129,8 +134,10 @@ def tile_fr_pb_t_kernel(
         sums = {}
         s_tile = {}
         own_bank = {}
-        scaled_tile = {}
-        u_bank = {}
+        own_tile = {}
+        t_bank = {}
+        co_tile = {}
+        back_bank = {}
         grouped_tile = {}
         re_codes = {}
         re_scales = {}
@@ -155,56 +162,50 @@ def tile_fr_pb_t_kernel(
                 ("fe0", extras[0]),
                 ("fe1", extras[1]),
             ):
-                raw[unit, name] = raw_pool.tile([P, SLOTS, HALF], BF16, name="raw_" + name)
-                nc.sync.dma_start(
-                    out=raw[unit, name][:], in_=view[n, :, :, h * HALF : (h + 1) * HALF]
-                )
+                tile = raw_pool.tile([P, SLOTS, HALF], BF16, name="raw_" + name)
+                for j in range(SLOTS):
+                    nc.sync.dma_start(
+                        out=tile[:, j, :],
+                        in_=view[n, j % 2, j // 2, :, :, h * HALF : (h + 1) * HALF],
+                    )
+                raw[unit, name] = tile
 
-        def gate_own(job):
+        def widen_group(job):
             if not starts(job, GROUP):
                 return
             unit, i, b = place(job)
-            column = IMAGES * i + unit // HALVES
-            gated_tile[job] = wide_pool.tile([P, SLOTS, HALF], F32, name="gated")
-            for j in range(SLOTS):
+            n = unit // HALVES
+            for kind, name in (("other", "x%d" % (1 - i)), ("extra", "fe%d" % i)):
+                tile = wide_pool.tile([P, SLOTS, HALF], F32, name="wide_%s%d" % (kind, i))
                 nc.gpsimd.tensor_scalar(
-                    out=gated_tile[job][:, j, :],
-                    in0=raw[unit, "x%d" % i][:, j, :],
-                    scalar1=gates[:, j, column : column + 1],
+                    out=tile[:],
+                    in0=raw[unit, name][:],
+                    scalar1=1.0,
                     scalar2=0.0,
                     op0=ALU.mult,
                     op1=ALU.add,
                 )
+                wide[unit, i, kind] = tile
+                if kind == "other":
+                    gated = wide_pool.tile([P, SLOTS, HALF], F32, name="wide_gated%d" % i)
+                    column = IMAGES * i + n
+                    for j in range(SLOTS):
+                        nc.gpsimd.tensor_scalar(
+                            out=gated[:, j, :],
+                            in0=raw[unit, "x%d" % i][:, j, :],
+                            scalar1=gates[:, j, column : column + 1],
+                            scalar2=0.0,
+                            op0=ALU.mult,
+                            op1=ALU.add,
+                        )
+                    wide[unit, i, "gated"] = gated
 
-        def widen_other(job):
-            if not starts(job, GROUP):
-                return
-            unit, i, b = place(job)
-            other_tile[job] = wide_pool.tile([P, SLOTS, HALF], F32, name="other")
-            nc.vector.tensor_copy(out=other_tile[job][:], in_=raw[unit, "x%d" % (1 - i)][:])
-
-        def add_rest(job):
-            if not starts(job, GROUP):
-                return
-            unit, i, b = place(job)
-            rest_tile[job] = wide_pool.tile([P, SLOTS, HALF], F32, name="rest")
-            nc.gpsimd.tensor_tensor(
-                out=rest_tile[job][:],
-                in0=raw[unit, "x%d" % (1 - i)][:],
-                in1=raw[unit, "fe%d" % i][:],
-                op=ALU.add,
-            )
-
-        def sum_r(job):
-            if not starts(job, 1):
-                return
-            b = job % GROUP
+        def sum_by_position(bank, first, second, b):
             columns = slice(b * BLOCK, (b + 1) * BLOCK)
-            bank = psum_r.tile([P, SLOTS, P], F32, name="r_ps")
             for j in range(SLOTS):
                 nc.tensor.matmul(
                     bank[:, j, :],
-                    lhsT=gated_tile[job - b][:, j, columns],
+                    lhsT=first[:, j, columns],
                     rhs=ident_f32[:],
                     is_transpose=True,
                     start=True,
@@ -212,12 +213,19 @@ def tile_fr_pb_t_kernel(
                 )
                 nc.tensor.matmul(
                     bank[:, j, :],
-                    lhsT=other_tile[job - b][:, j, columns],
+                    lhsT=second[:, j, columns],
                     rhs=ident_f32[:],
                     is_transpose=True,
                     start=False,
                     stop=True,
                 )
+
+        def sum_r(job):
+            if not starts(job, 1):
+                return
+            unit, i, b = place(job)
+            bank = psum_r.tile([P, SLOTS, P], F32, name="r_ps")
+            sum_by_position(bank, wide[unit, i, "gated"], wide[unit, i, "other"], b)
             r_bank[job] = bank[:].rearrange("q j c -> q (j c)")
 
         def exp_a(job):
@@ -278,7 +286,7 @@ def tile_fr_pb_t_kernel(
             if not starts(job, PAIR):
                 return
             unit, i, b = place(job)
-            own_bank[job] = psum_own.tile([P, PAIR, CHANNELS], BF16, name="own_ps")
+            own_bank[job] = psum_one.tile([P, PAIR, CHANNELS], BF16, name="own_ps", tag="own")
             for k in range(PAIR):
                 for j in range(SLOTS):
                     nc.tensor.transpose(
@@ -287,39 +295,65 @@ def tile_fr_pb_t_kernel(
                         ident_bf16[:],
                     )
 
-        def scale_own(job):
-            if not starts(job, 1):
+        def own_copy(job):
+            if not starts(job, PAIR):
                 return
-            group, b = divmod(job, GROUP)
-            scaled_tile[job] = work.tile([P, SLOTS, P], F32, name="scaled")
-            nc.scalar.activation(
-                out=scaled_tile[job][:].rearrange("q j c -> q (j c)"),
-                in_=own_bank[job - job % PAIR][:, job % PAIR, :],
-                func=ACT.Copy,
-                scale=s_tile[group][:, b : b + 1],
-            )
+            own_tile[job] = work.tile([P, PAIR, CHANNELS], BF16, name="own")
+            nc.scalar.copy(out=own_tile[job][:], in_=own_bank[job][:])
 
-        def turn_back(job):
+        def sum_t(job):
             if not starts(job, 1):
                 return
-            u_bank[job] = psum_u.tile([P, SLOTS, BLOCK], F32, name="u_ps")
-            for j in range(SLOTS):
-                nc.tensor.transpose(u_bank[job][:, j, :], scaled_tile[job][:, j, :], ident_f32[:])
+            unit, i, b = place(job)
+            bank = psum_t.tile([P, SLOTS, P], F32, name="t_ps")
+            sum_by_position(bank, wide[unit, i, "other"], wide[unit, i, "extra"], b)
+            t_bank[job] = bank[:].rearrange("q j c -> q (j c)")
 
         def fuse(job):
             if not starts(job, 1):
+                return
+            group, b = divmod(job, GROUP)
+            co_tile[job] = work.tile([P, CHANNELS], BF16, name="co")
+            nc.vector.scalar_tensor_tensor(
+                out=co_tile[job][:],
+                in0=own_tile[job - job % PAIR][:, job % PAIR, :],
+                scalar=s_tile[group][:, b : b + 1],
+                in1=t_bank[job],
+                op0=ALU.mult,
+                op1=ALU.add,
+            )
+
+        def back_transposes(job):
+            if not starts(job, 1):
+                return
+            k = job % PAIR
+            if k == 0:
+                back_bank[job] = psum_one.tile([P, 2, PAIR * BLOCK], F32, name="back_ps", tag="back")
+            co_words = co_tile[job][:].bitcast(F32)
+            for u in range(2):
+                nc.tensor.transpose(
+                    back_bank[job - k][:, u, k * BLOCK : (k + 1) * BLOCK],
+                    co_words[:, u * P : (u + 1) * P],
+                    ident_f32[:],
+                )
+
+        def back_copy(job):
+            if not starts(job, PAIR):
                 return
             group, b = divmod(job, GROUP)
             if b == 0:
                 grouped_tile[group] = mx_pool.tile(
                     [P, HALF, SLOTS], BF16, name="grouped", align_bytes=64
                 )
-            columns = slice(b * BLOCK, (b + 1) * BLOCK)
-            nc.vector.tensor_tensor(
-                out=grouped_tile[group][:, columns, :],
-                in0=u_bank[job][:].rearrange("p j w -> p w j"),
-                in1=rest_tile[job - b][:, :, columns].rearrange("p j w -> p w j"),
-                op=ALU.add,
+            grouped_words = (
+                grouped_tile[group][:]
+                .rearrange("q w t -> q (w t)")
+                .bitcast(F32)
+                .rearrange("q (w u) -> q w u", u=2)
+            )
+            nc.scalar.copy(
+                out=grouped_words[:, b * BLOCK : (b + PAIR) * BLOCK, :],
+                in_=back_bank[job][:].rearrange("q u w -> q w u"),
             )
 
         def quantise(job):
@@ -332,24 +366,24 @@ def tile_fr_pb_t_kernel(
             nc.vector.quantize_mx(
                 out=re_codes[unit][:, i, :].bitcast(FP8X4),
                 scales=re_scales[unit][:, i, :],
-                in_=grouped_tile[job // GROUP][:].rearrange("p w j -> p (w j)"),
+                in_=grouped_tile[job // GROUP][:].rearrange("q w t -> q (w t)"),
             )
 
-        def project(job, w):
+        def project(job, w, g):
             if not starts(job, UNIT):
                 return
             unit = job // UNIT
-            po_bank[unit, w] = psum_po.tile([P, HALF], F32, name="po_ps")
-            for g in range(2):
-                nc.tensor.matmul_mx(
-                    out=po_bank[unit, w][:],
-                    lhsT=w_words[:, w, g, :].bitcast(FP8X4),
-                    lhsT_scale=w_scales[:, w, g, :],
-                    rhs=re_codes[unit][:, g, :].bitcast(FP8X4),
-                    rhs_scale=re_scales[unit][:, g, :],
-                    start=(g == 0),
-                    stop=(g == 1),
-                )
+            if g == 0:
+                po_bank[unit, w] = psum_one.tile([P, HALF], F32, name="po_ps", tag="po")
+            nc.tensor.matmul_mx(
+                out=po_bank[unit, w][:],
+                lhsT=w_words[:, w, g, :].bitcast(FP8X4),
+                lhsT_scale=w_scales[:, w, g, :],
+                rhs=re_codes[unit][:, g, :].bitcast(FP8X4),
+                rhs_scale=re_scales[unit][:, g, :],
+                start=(g == 0),
+                stop=(g == 1),
+            )
 
         def add_bias_and_store(job, w):
             if not starts(job, UNIT):
@@ -367,22 +401,24 @@ def tile_fr_pb_t_kernel(
             nc.sync.dma_start(out=outs[w][n, :, h * HALF : (h + 1) * HALF], in_=po[:])
 
         with tc.manual_schedule():
-            for t in range(-12, JOBS + 19):
+            for t in range(-12, JOBS + 23):
                 load_unit(t + 12)
-                gate_own(t + 8)
-                add_rest(t + 1)
-                fuse(t - 7)
+                widen_group(t + 8)
+                fuse(t - 5)
                 sum_r(t + 1)
                 exp_a(t)
                 exp_e(t - 1)
                 find_max(t)
                 sum_er(t - 1)
-                scale_own(t - 5)
-                turn_back(t - 6)
-                own_transposes(t - 4)
+                sum_t(t - 4)
+                own_transposes(t - 3)
+                own_copy(t - 4)
+                back_copy(t - 7)
+                back_transposes(t - 5)
                 quantise(t - 10)
-                widen_other(t + 5)
-                project(t - 15, 0)
-                add_bias_and_store(t - 16, 0)
-                project(t - 17, 1)
-                add_bias_and_store(t - 18, 1)
+                project(t - 15, 0, 0)
+                project(t - 17, 0, 1)
+                add_bias_and_store(t - 18, 0)
+                project(t - 19, 1, 0)
+                project(t - 21, 1, 1)
+                add_bias_and_store(t - 22, 1)

@@ -132,6 +132,7 @@ def tile_fr_pb_t_kernel(
         minus_max = {}
         e_tile = {}
         sums = {}
+        one_over = {}
         s_tile = {}
         own_bank = {}
         own_tile = {}
@@ -258,29 +259,29 @@ def tile_fr_pb_t_kernel(
                 accum_out=sums[group, "e"][:, b : b + 1],
             )
 
+        def invert(job):
+            if not starts(job, 1):
+                return
+            group, b = divmod(job, GROUP)
+            one_over[job] = small.tile([P, 1], F32, name="one_over")
+            nc.vector.reciprocal(out=one_over[job][:], in_=sums[group, "e"][:, b : b + 1])
+
         def sum_er(job):
             if not starts(job, 1):
                 return
             group, b = divmod(job, GROUP)
             if b == 0:
-                sums[group, "er"] = small.tile([P, GROUP], F32, name="sum_er")
+                s_tile[group] = small.tile([P, GROUP], F32, name="s")
             products = work.tile([P, CHANNELS], BF16, name="products")
             nc.vector.scalar_tensor_tensor(
                 out=products[:],
                 in0=e_tile[job][:],
-                scalar=1.0,
+                scalar=one_over[job][:, 0:1],
                 in1=r_bank[job],
                 op0=ALU.mult,
                 op1=ALU.mult,
-                accum_out=sums[group, "er"][:, b : b + 1],
+                accum_out=s_tile[group][:, b : b + 1],
             )
-            if b == GROUP - 1:
-                one_over = small.tile([P, GROUP], F32, name="one_over")
-                nc.vector.reciprocal(out=one_over[:], in_=sums[group, "e"][:])
-                s_tile[group] = small.tile([P, GROUP], F32, name="s")
-                nc.vector.tensor_mul(
-                    out=s_tile[group][:], in0=sums[group, "er"][:], in1=one_over[:]
-                )
 
         def own_transposes(job):
             if not starts(job, PAIR):
@@ -404,11 +405,12 @@ def tile_fr_pb_t_kernel(
             for t in range(-12, JOBS + 23):
                 load_unit(t + 12)
                 widen_group(t + 8)
-                fuse(t - 5)
                 sum_r(t + 1)
                 exp_a(t)
                 exp_e(t - 1)
                 find_max(t)
+                invert(t - 1)
+                fuse(t - 5)
                 sum_er(t - 1)
                 sum_t(t - 4)
                 own_transposes(t - 3)

@@ -70,7 +70,8 @@ def tile_fr_pb_t_kernel(
         small = ctx.enter_context(tc.tile_pool(name="small", bufs=4))
         mx_pool = ctx.enter_context(tc.tile_pool(name="mx", bufs=2))
         out_pool = ctx.enter_context(tc.tile_pool(name="outp", bufs=4))
-        psum_r = ctx.enter_context(tc.psum_pool(name="psum_r", bufs=3))
+        co_pool = ctx.enter_context(tc.tile_pool(name="co", bufs=6))
+        psum_r = ctx.enter_context(tc.psum_pool(name="psum_r", bufs=4))
         psum_t = ctx.enter_context(tc.psum_pool(name="psum_t", bufs=2))
         psum_one = ctx.enter_context(tc.psum_pool(name="psum_one", bufs=1))
 
@@ -225,7 +226,7 @@ def tile_fr_pb_t_kernel(
             if not starts(job, 1):
                 return
             unit, i, b = place(job)
-            bank = psum_r.tile([P, SLOTS, P], F32, name="r_ps")
+            bank = psum_r.tile([P, SLOTS, P], F32, name="r_ps", tag="r")
             sum_by_position(bank, wide[unit, i, "gated"], wide[unit, i, "other"], b)
             r_bank[job] = bank[:].rearrange("q j c -> q (j c)")
 
@@ -314,7 +315,7 @@ def tile_fr_pb_t_kernel(
             if not starts(job, 1):
                 return
             group, b = divmod(job, GROUP)
-            co_tile[job] = work.tile([P, CHANNELS], BF16, name="co")
+            co_tile[job] = co_pool.tile([P, CHANNELS], BF16, name="co")
             nc.vector.scalar_tensor_tensor(
                 out=co_tile[job][:],
                 in0=own_tile[job - job % PAIR][:, job % PAIR, :],
@@ -325,18 +326,17 @@ def tile_fr_pb_t_kernel(
             )
 
         def back_transposes(job):
-            if not starts(job, 1):
+            if not starts(job, PAIR):
                 return
-            k = job % PAIR
-            if k == 0:
-                back_bank[job] = psum_one.tile([P, 2, PAIR * BLOCK], F32, name="back_ps", tag="back")
-            co_words = co_tile[job][:].bitcast(F32)
-            for u in range(2):
-                nc.tensor.transpose(
-                    back_bank[job - k][:, u, k * BLOCK : (k + 1) * BLOCK],
-                    co_words[:, u * P : (u + 1) * P],
-                    ident_f32[:],
-                )
+            back_bank[job] = psum_one.tile([P, 2, PAIR * BLOCK], F32, name="back_ps", tag="back")
+            for k in range(PAIR):
+                co_words = co_tile[job + k][:].bitcast(F32)
+                for u in range(2):
+                    nc.tensor.transpose(
+                        back_bank[job][:, u, k * BLOCK : (k + 1) * BLOCK],
+                        co_words[:, u * P : (u + 1) * P],
+                        ident_f32[:],
+                    )
 
         def back_copy(job):
             if not starts(job, PAIR):
@@ -375,7 +375,7 @@ def tile_fr_pb_t_kernel(
                 return
             unit = job // UNIT
             if g == 0:
-                po_bank[unit, w] = psum_one.tile([P, HALF], F32, name="po_ps", tag="po")
+                po_bank[unit, w] = psum_r.tile([P, HALF], F32, name="po_ps", tag="r")
             nc.tensor.matmul_mx(
                 out=po_bank[unit, w][:],
                 lhsT=w_words[:, w, g, :].bitcast(FP8X4),
@@ -402,25 +402,25 @@ def tile_fr_pb_t_kernel(
             nc.sync.dma_start(out=outs[w][n, :, h * HALF : (h + 1) * HALF], in_=po[:])
 
         with tc.manual_schedule():
-            for t in range(-12, JOBS + 23):
-                load_unit(t + 12)
-                widen_group(t + 8)
-                sum_r(t + 1)
-                exp_a(t)
-                exp_e(t - 1)
+            for t in range(-16, JOBS + 24):
+                load_unit(t + 16)
+                widen_group(t + 10)
+                sum_r(t + 2)
                 find_max(t)
+                exp_a(t + 1)
+                exp_e(t)
                 invert(t - 1)
-                fuse(t - 5)
                 sum_er(t - 1)
-                sum_t(t - 4)
-                own_transposes(t - 3)
-                own_copy(t - 4)
-                back_copy(t - 7)
-                back_transposes(t - 5)
-                quantise(t - 10)
-                project(t - 15, 0, 0)
-                project(t - 17, 0, 1)
-                add_bias_and_store(t - 18, 0)
-                project(t - 19, 1, 0)
-                project(t - 21, 1, 1)
-                add_bias_and_store(t - 22, 1)
+                fuse(t - 4)
+                sum_t(t - 3)
+                own_transposes(t - 1)
+                own_copy(t - 2)
+                back_transposes(t - 7)
+                back_copy(t - 8)
+                quantise(t - 12)
+                project(t - 18, 0, 0)
+                project(t - 18, 0, 1)
+                add_bias_and_store(t - 19, 0)
+                project(t - 22, 1, 0)
+                project(t - 22, 1, 1)
+                add_bias_and_store(t - 23, 1)

@@ -71,6 +71,7 @@ def tile_fr_pb_t_kernel(
         mx_pool = ctx.enter_context(tc.tile_pool(name="mx", bufs=2))
         out_pool = ctx.enter_context(tc.tile_pool(name="outp", bufs=4))
         co_pool = ctx.enter_context(tc.tile_pool(name="co", bufs=6))
+        own_pool = ctx.enter_context(tc.tile_pool(name="own", bufs=5))
         psum_r = ctx.enter_context(tc.psum_pool(name="psum_r", bufs=4))
         psum_t = ctx.enter_context(tc.psum_pool(name="psum_t", bufs=2))
         psum_one = ctx.enter_context(tc.psum_pool(name="psum_one", bufs=1))
@@ -101,30 +102,34 @@ def tile_fr_pb_t_kernel(
 
         bias_rows = const.tile([P, P], BF16)
         nc.vector.memset(bias_rows[:], 0.0)
-        nc.sync.dma_start(out=bias_rows[0:1, :], in_=p1_b.rearrange("(r o) -> r o", r=1))
-        nc.sync.dma_start(out=bias_rows[1:2, :], in_=p2_b.rearrange("(r o) -> r o", r=1))
-        bias_ps = psum_one.tile([P, P], BF16, tag="back")
-        nc.tensor.transpose(bias_ps[:], bias_rows[:], ident_bf16[:])
         biases = const.tile([P, 2], F32)
-        nc.vector.tensor_copy(out=biases[:], in_=bias_ps[:, 0:2])
 
         w_words = const.tile([P, 2, 2, OUT_CHANNELS], U32, align_bytes=64)
         w_scales = const.tile([P, 2, 2, OUT_CHANNELS], U8, align_bytes=64)
         nc.vector.memset(w_scales[:].bitcast(I32), 0)
-        for w, (words, scales) in enumerate(
-            ((p1_w_words, p1_w_scales), (p2_w_words, p2_w_scales))
-        ):
-            nc.sync.dma_start(
-                out=w_words[:, w].bitcast(I32),
-                in_=words.rearrange("g p n t -> p g (n t)").bitcast(I32),
-            )
-            for quadrant in range(4):
+
+        def load_weights(job):
+            if job != 0:
+                return
+            nc.sync.dma_start(out=bias_rows[0:1, :], in_=p1_b.rearrange("(r o) -> r o", r=1))
+            nc.sync.dma_start(out=bias_rows[1:2, :], in_=p2_b.rearrange("(r o) -> r o", r=1))
+            bias_ps = psum_one.tile([P, P], BF16, tag="back")
+            nc.tensor.transpose(bias_ps[:], bias_rows[:], ident_bf16[:])
+            nc.vector.tensor_copy(out=biases[:], in_=bias_ps[:, 0:2])
+            for w, (words, scales) in enumerate(
+                ((p1_w_words, p1_w_scales), (p2_w_words, p2_w_scales))
+            ):
                 nc.sync.dma_start(
-                    out=w_scales[32 * quadrant : 32 * quadrant + 4, w].bitcast(I32),
-                    in_=scales[:, 4 * quadrant : 4 * quadrant + 4, :]
-                    .rearrange("g q n -> q g n")
-                    .bitcast(I32),
+                    out=w_words[:, w].bitcast(I32),
+                    in_=words.rearrange("g p n t -> p g (n t)").bitcast(I32),
                 )
+                for quadrant in range(4):
+                    nc.sync.dma_start(
+                        out=w_scales[32 * quadrant : 32 * quadrant + 4, w].bitcast(I32),
+                        in_=scales[:, 4 * quadrant : 4 * quadrant + 4, :]
+                        .rearrange("g q n -> q g n")
+                        .bitcast(I32),
+                    )
 
         raw = {}
         wide = {}
@@ -261,27 +266,40 @@ def tile_fr_pb_t_kernel(
             )
 
         def invert(job):
+            if not starts(job, GROUP):
+                return
+            group = job // GROUP
+            one_over[group] = small.tile([P, GROUP], F32, name="one_over")
+            nc.vector.reciprocal(out=one_over[group][:], in_=sums[group, "e"][:])
+
+        def divide(job):
             if not starts(job, 1):
                 return
             group, b = divmod(job, GROUP)
-            one_over[job] = small.tile([P, 1], F32, name="one_over")
-            nc.vector.reciprocal(out=one_over[job][:], in_=sums[group, "e"][:, b : b + 1])
+            if b == 0:
+                s_tile[group] = small.tile([P, GROUP], F32, name="s")
+            nc.scalar.activation(
+                out=s_tile[group][:, b : b + 1],
+                in_=sums[group, "er"][:, b : b + 1],
+                func=ACT.Copy,
+                scale=one_over[group][:, b : b + 1],
+            )
 
         def sum_er(job):
             if not starts(job, 1):
                 return
             group, b = divmod(job, GROUP)
             if b == 0:
-                s_tile[group] = small.tile([P, GROUP], F32, name="s")
+                sums[group, "er"] = small.tile([P, GROUP], F32, name="sum_er")
             products = work.tile([P, CHANNELS], BF16, name="products")
             nc.vector.scalar_tensor_tensor(
                 out=products[:],
                 in0=e_tile[job][:],
-                scalar=one_over[job][:, 0:1],
+                scalar=1.0,
                 in1=r_bank[job],
                 op0=ALU.mult,
                 op1=ALU.mult,
-                accum_out=s_tile[group][:, b : b + 1],
+                accum_out=sums[group, "er"][:, b : b + 1],
             )
 
         def own_transposes(job):
@@ -300,7 +318,7 @@ def tile_fr_pb_t_kernel(
         def own_copy(job):
             if not starts(job, PAIR):
                 return
-            own_tile[job] = work.tile([P, PAIR, CHANNELS], BF16, name="own")
+            own_tile[job] = own_pool.tile([P, PAIR, CHANNELS], BF16, name="own")
             nc.scalar.copy(out=own_tile[job][:], in_=own_bank[job][:])
 
         def sum_t(job):
@@ -402,25 +420,27 @@ def tile_fr_pb_t_kernel(
             nc.sync.dma_start(out=outs[w][n, :, h * HALF : (h + 1) * HALF], in_=po[:])
 
         with tc.manual_schedule():
-            for t in range(-16, JOBS + 24):
+            for t in range(-16, JOBS + 27):
                 load_unit(t + 16)
+                load_weights(t + 15)
                 widen_group(t + 10)
                 sum_r(t + 2)
                 find_max(t)
                 exp_a(t + 1)
                 exp_e(t)
-                invert(t - 1)
                 sum_er(t - 1)
-                fuse(t - 4)
-                sum_t(t - 3)
+                invert(t - 4)
+                divide(t - 5)
+                fuse(t - 7)
+                sum_t(t - 6)
                 own_transposes(t - 1)
                 own_copy(t - 2)
-                back_transposes(t - 7)
-                back_copy(t - 8)
-                quantise(t - 12)
-                project(t - 18, 0, 0)
-                project(t - 18, 0, 1)
-                add_bias_and_store(t - 19, 0)
-                project(t - 22, 1, 0)
-                project(t - 22, 1, 1)
-                add_bias_and_store(t - 23, 1)
+                back_transposes(t - 10)
+                back_copy(t - 11)
+                quantise(t - 15)
+                project(t - 21, 0, 0)
+                project(t - 21, 0, 1)
+                add_bias_and_store(t - 22, 0)
+                project(t - 25, 1, 0)
+                project(t - 25, 1, 1)
+                add_bias_and_store(t - 26, 1)

@@ -164,8 +164,8 @@ def tile_fr_pb_t_kernel(
             unit = job // UNIT
             n, h = divmod(unit, HALVES)
             for name, view in (
-                ("x0", streams[0]),
                 ("x1", streams[1]),
+                ("x0", streams[0]),
                 ("fe0", extras[0]),
                 ("fe1", extras[1]),
             ):
@@ -177,35 +177,50 @@ def tile_fr_pb_t_kernel(
                     )
                 raw[unit, name] = tile
 
-        def widen_group(job):
+        def widen(unit, i, kind, name):
+            tile = wide_pool.tile([P, SLOTS, HALF], F32, name="wide_%s%d" % (kind, i))
+            nc.gpsimd.tensor_scalar(
+                out=tile[:],
+                in0=raw[unit, name][:],
+                scalar1=1.0,
+                scalar2=0.0,
+                op0=ALU.mult,
+                op1=ALU.add,
+            )
+            wide[unit, i, kind] = tile
+
+        def widen_for_r(job):
             if not starts(job, GROUP):
                 return
             unit, i, b = place(job)
             n = unit // HALVES
-            for kind, name in (("other", "x%d" % (1 - i)), ("extra", "fe%d" % i)):
-                tile = wide_pool.tile([P, SLOTS, HALF], F32, name="wide_%s%d" % (kind, i))
-                nc.gpsimd.tensor_scalar(
-                    out=tile[:],
-                    in0=raw[unit, name][:],
-                    scalar1=1.0,
-                    scalar2=0.0,
-                    op0=ALU.mult,
-                    op1=ALU.add,
-                )
-                wide[unit, i, kind] = tile
-                if kind == "other":
-                    gated = wide_pool.tile([P, SLOTS, HALF], F32, name="wide_gated%d" % i)
-                    column = IMAGES * i + n
-                    for j in range(SLOTS):
-                        nc.gpsimd.tensor_scalar(
-                            out=gated[:, j, :],
-                            in0=raw[unit, "x%d" % i][:, j, :],
-                            scalar1=gates[:, j, column : column + 1],
-                            scalar2=0.0,
-                            op0=ALU.mult,
-                            op1=ALU.add,
-                        )
-                    wide[unit, i, "gated"] = gated
+            widen(unit, i, "other", "x%d" % (1 - i))
+            gated = wide_pool.tile([P, SLOTS, HALF], F32, name="wide_gated%d" % i)
+            column = IMAGES * i + n
+            for j in range(SLOTS):
+                if job == 0:
+                    nc.scalar.activation(
+                        out=gated[:, j, :],
+                        in_=raw[unit, "x%d" % i][:, j, :],
+                        func=ACT.Copy,
+                        scale=gates[:, j, column : column + 1],
+                    )
+                else:
+                    nc.gpsimd.tensor_scalar(
+                        out=gated[:, j, :],
+                        in0=raw[unit, "x%d" % i][:, j, :],
+                        scalar1=gates[:, j, column : column + 1],
+                        scalar2=0.0,
+                        op0=ALU.mult,
+                        op1=ALU.add,
+                    )
+            wide[unit, i, "gated"] = gated
+
+        def widen_extra(job):
+            if not starts(job, GROUP):
+                return
+            unit, i, b = place(job)
+            widen(unit, i, "extra", "fe%d" % i)
 
         def sum_by_position(bank, first, second, b):
             columns = slice(b * BLOCK, (b + 1) * BLOCK)
@@ -423,7 +438,8 @@ def tile_fr_pb_t_kernel(
             for t in range(-16, JOBS + 27):
                 load_unit(t + 16)
                 load_weights(t + 15)
-                widen_group(t + 10)
+                widen_for_r(t + 10)
+                widen_extra(t + 6)
                 sum_r(t + 2)
                 find_max(t)
                 exp_a(t + 1)

@@ -97,8 +97,13 @@ def tile_fr_pb_t_kernel(
         gate_ps = psum_one.tile([P, SLOTS, P], BF16, tag="own")
         for j in range(SLOTS):
             nc.tensor.transpose(gate_ps[:, j, :], gate_sorted[:, j, :], ident_bf16[:])
-        gates = const.tile([P, SLOTS, P], F32)
-        nc.scalar.activation(out=gates[:], in_=gate_ps[:], func=ACT.Sigmoid)
+        gates = const.tile([P, SLOTS, 2 * IMAGES], F32)
+        nc.scalar.activation(
+            out=gates[:], in_=gate_ps[:, :, 0 : 2 * IMAGES], func=ACT.Tanh, scale=0.5
+        )
+        nc.vector.tensor_scalar(
+            out=gates[:], in0=gates[:], scalar1=0.5, scalar2=0.5, op0=ALU.mult, op1=ALU.add
+        )
 
         bias_rows = const.tile([P, P], BF16)
         nc.vector.memset(bias_rows[:], 0.0)
@@ -113,9 +118,6 @@ def tile_fr_pb_t_kernel(
                 return
             nc.sync.dma_start(out=bias_rows[0:1, :], in_=p1_b.rearrange("(r o) -> r o", r=1))
             nc.sync.dma_start(out=bias_rows[1:2, :], in_=p2_b.rearrange("(r o) -> r o", r=1))
-            bias_ps = psum_one.tile([P, P], BF16, tag="back")
-            nc.tensor.transpose(bias_ps[:], bias_rows[:], ident_bf16[:])
-            nc.vector.tensor_copy(out=biases[:], in_=bias_ps[:, 0:2])
             for w, (words, scales) in enumerate(
                 ((p1_w_words, p1_w_scales), (p2_w_words, p2_w_scales))
             ):
@@ -130,6 +132,13 @@ def tile_fr_pb_t_kernel(
                         .rearrange("g q n -> q g n")
                         .bitcast(I32),
                     )
+
+        def turn_biases(job):
+            if job != 0:
+                return
+            bias_ps = psum_one.tile([P, P], BF16, name="bias_ps", tag="back")
+            nc.tensor.transpose(bias_ps[:], bias_rows[:], ident_bf16[:])
+            nc.vector.tensor_copy(out=biases[:], in_=bias_ps[:, 0:2])
 
         raw = {}
         wide = {}
@@ -177,52 +186,59 @@ def tile_fr_pb_t_kernel(
                     )
                 raw[unit, name] = tile
 
-        def widen(unit, i, kind, name):
-            tile = wide_pool.tile([P, SLOTS, HALF], F32, name="wide_%s%d" % (kind, i))
+        def widen(tile, source, columns, slots=SLOTS):
             nc.gpsimd.tensor_scalar(
-                out=tile[:],
-                in0=raw[unit, name][:],
+                out=tile[:, 0:slots, columns],
+                in0=source[:, 0:slots, columns],
                 scalar1=1.0,
                 scalar2=0.0,
                 op0=ALU.mult,
                 op1=ALU.add,
             )
-            wide[unit, i, kind] = tile
+
+        def gate(tile, source, i, n, columns, on_scalar):
+            column = IMAGES * i + n
+            for j in range(SLOTS):
+                out, in0 = tile[:, j, columns], source[:, j, columns]
+                factor = gates[:, j, column : column + 1]
+                if on_scalar:
+                    nc.scalar.activation(out=out, in_=in0, func=ACT.Copy, scale=factor)
+                else:
+                    nc.gpsimd.tensor_scalar(
+                        out=out, in0=in0, scalar1=factor, scalar2=0.0, op0=ALU.mult, op1=ALU.add
+                    )
 
         def widen_for_r(job):
             if not starts(job, GROUP):
                 return
             unit, i, b = place(job)
             n = unit // HALVES
-            widen(unit, i, "other", "x%d" % (1 - i))
-            gated = wide_pool.tile([P, SLOTS, HALF], F32, name="wide_gated%d" % i)
-            column = IMAGES * i + n
-            for j in range(SLOTS):
-                if job == 0:
-                    nc.scalar.activation(
-                        out=gated[:, j, :],
-                        in_=raw[unit, "x%d" % i][:, j, :],
-                        func=ACT.Copy,
-                        scale=gates[:, j, column : column + 1],
-                    )
-                else:
-                    nc.gpsimd.tensor_scalar(
-                        out=gated[:, j, :],
-                        in0=raw[unit, "x%d" % i][:, j, :],
-                        scalar1=gates[:, j, column : column + 1],
-                        scalar2=0.0,
-                        op0=ALU.mult,
-                        op1=ALU.add,
-                    )
-            wide[unit, i, "gated"] = gated
+            other, own = raw[unit, "x%d" % (1 - i)], raw[unit, "x%d" % i]
+            wide[unit, i, "other"] = wide_pool.tile([P, SLOTS, HALF], F32, name="wide_other%d" % i)
+            wide[unit, i, "gated"] = wide_pool.tile([P, SLOTS, HALF], F32, name="wide_gated%d" % i)
+            first = job == 0
+            size = HALF // 2 if first else HALF
+            for start in range(0, HALF, size):
+                columns = slice(start, start + size)
+                widen(wide[unit, i, "other"], other, columns)
+                gate(wide[unit, i, "gated"], own, i, n, columns, on_scalar=first)
+
+        def plain_slot(unit, i):
+            return i == 0 or unit % 2 == 1
 
         def widen_extra(job):
             if not starts(job, GROUP):
                 return
             unit, i, b = place(job)
-            widen(unit, i, "extra", "fe%d" % i)
+            wide[unit, i, "extra"] = wide_pool.tile([P, SLOTS, HALF], F32, name="wide_extra%d" % i)
+            widen(
+                wide[unit, i, "extra"],
+                raw[unit, "fe%d" % i],
+                slice(0, HALF),
+                SLOTS - 1 if plain_slot(unit, i) else SLOTS,
+            )
 
-        def sum_by_position(bank, first, second, b):
+        def sum_by_position(bank, first, second, b, last=None):
             columns = slice(b * BLOCK, (b + 1) * BLOCK)
             for j in range(SLOTS):
                 nc.tensor.matmul(
@@ -233,6 +249,15 @@ def tile_fr_pb_t_kernel(
                     start=True,
                     stop=False,
                 )
+                if last is not None and j == SLOTS - 1:
+                    nc.tensor.matmul(
+                        bank[:, j, :],
+                        lhsT=last[:, j, columns],
+                        rhs=ident_bf16[:],
+                        start=False,
+                        stop=True,
+                    )
+                    continue
                 nc.tensor.matmul(
                     bank[:, j, :],
                     lhsT=second[:, j, columns],
@@ -341,7 +366,8 @@ def tile_fr_pb_t_kernel(
                 return
             unit, i, b = place(job)
             bank = psum_t.tile([P, SLOTS, P], F32, name="t_ps")
-            sum_by_position(bank, wide[unit, i, "other"], wide[unit, i, "extra"], b)
+            last = raw[unit, "fe%d" % i] if plain_slot(unit, i) else None
+            sum_by_position(bank, wide[unit, i, "other"], wide[unit, i, "extra"], b, last)
             t_bank[job] = bank[:].rearrange("q j c -> q (j c)")
 
         def fuse(job):
@@ -438,6 +464,7 @@ def tile_fr_pb_t_kernel(
             for t in range(-16, JOBS + 27):
                 load_unit(t + 16)
                 load_weights(t + 15)
+                turn_biases(t - 4)
                 widen_for_r(t + 10)
                 widen_extra(t + 6)
                 sum_r(t + 2)

@@ -434,7 +434,7 @@ def tile_fr_pb_t_kernel(
                 return
             unit = job // UNIT
             if g == 0:
-                po_bank[unit, w] = psum_r.tile([P, HALF], F32, name="po_ps", tag="r")
+                po_bank[unit, w] = psum_one.tile([P, HALF], F32, name="po_ps", tag="own")
             nc.tensor.matmul_mx(
                 out=po_bank[unit, w][:],
                 lhsT=w_words[:, w, g, :].bitcast(FP8X4),
@@ -467,6 +467,11 @@ def tile_fr_pb_t_kernel(
                 turn_biases(t - 4)
                 widen_for_r(t + 10)
                 widen_extra(t + 6)
+                own_transposes(t - 2)
+                project(t - 21, 0, 0)
+                project(t - 21, 0, 1)
+                project(t - 23, 1, 0)
+                project(t - 23, 1, 1)
                 sum_r(t + 2)
                 find_max(t)
                 exp_a(t + 1)
@@ -476,14 +481,9 @@ def tile_fr_pb_t_kernel(
                 divide(t - 5)
                 fuse(t - 7)
                 sum_t(t - 6)
-                own_transposes(t - 1)
-                own_copy(t - 2)
                 back_transposes(t - 10)
                 back_copy(t - 11)
                 quantise(t - 15)
-                project(t - 21, 0, 0)
-                project(t - 21, 0, 1)
-                add_bias_and_store(t - 22, 0)
-                project(t - 25, 1, 0)
-                project(t - 25, 1, 1)
-                add_bias_and_store(t - 26, 1)
+                own_copy(t - 2)
+                add_bias_and_store(t - 21, 0)
+                add_bias_and_store(t - 23, 1)

@@ -246,25 +246,18 @@ def tile_fr_pb_t_kernel(
                     lhsT=first[:, j, columns],
                     rhs=ident_f32[:],
                     is_transpose=True,
-                    start=True,
+                    start=(j == 0),
                     stop=False,
                 )
-                if last is not None and j == SLOTS - 1:
-                    nc.tensor.matmul(
-                        bank[:, j, :],
-                        lhsT=last[:, j, columns],
-                        rhs=ident_bf16[:],
-                        start=False,
-                        stop=True,
-                    )
-                    continue
+            for j in range(SLOTS):
+                plain = last is not None and j == SLOTS - 1
                 nc.tensor.matmul(
                     bank[:, j, :],
-                    lhsT=second[:, j, columns],
-                    rhs=ident_f32[:],
-                    is_transpose=True,
+                    lhsT=(last if plain else second)[:, j, columns],
+                    rhs=(ident_bf16 if plain else ident_f32)[:],
+                    is_transpose=not plain,
                     start=False,
-                    stop=True,
+                    stop=(j == SLOTS - 1),
                 )
 
         def sum_r(job):

@@ -24,6 +24,7 @@ HALVES = POSITIONS // HALF
 BLOCK = 128
 BLOCKS = HALF // BLOCK
 PAIR = 2
+PAIRS = BLOCKS // PAIR
 GROUP = BLOCKS
 UNIT = 2 * GROUP
 JOBS = IMAGES * HALVES * UNIT
@@ -186,20 +187,27 @@ def tile_fr_pb_t_kernel(
                     )
                 raw[unit, name] = tile
 
-        def widen(tile, source, columns, slots=SLOTS):
+        def by_block(row):
+            return row.rearrange("p (h w k) -> p h k w", w=BLOCK, k=PAIR)
+
+        def new_wide(name):
+            return wide_pool.tile([P, SLOTS, PAIRS, PAIR, BLOCK], F32, name="wide_" + name)
+
+        def widen(tile, source, pair=None, slots=SLOTS):
+            if pair is None:
+                out = tile[:, 0:slots].rearrange("p j h k w -> p (j h) k w")
+                in0 = by_block(source[:, 0:slots].rearrange("p j s -> p (j s)"))
+            else:
+                out = tile[:, :, pair]
+                in0 = source[:].rearrange("p j (h w k) -> p j h k w", w=BLOCK, k=PAIR)[:, :, pair]
             nc.gpsimd.tensor_scalar(
-                out=tile[:, 0:slots, columns],
-                in0=source[:, 0:slots, columns],
-                scalar1=1.0,
-                scalar2=0.0,
-                op0=ALU.mult,
-                op1=ALU.add,
+                out=out, in0=in0, scalar1=1.0, scalar2=0.0, op0=ALU.mult, op1=ALU.add
             )
 
-        def gate(tile, source, i, n, columns, on_scalar):
+        def gate(tile, source, i, n, pairs, on_scalar):
             column = IMAGES * i + n
             for j in range(SLOTS):
-                out, in0 = tile[:, j, columns], source[:, j, columns]
+                out, in0 = tile[:, j, pairs], by_block(source[:, j, :])[:, pairs]
                 factor = gates[:, j, column : column + 1]
                 if on_scalar:
                     nc.scalar.activation(out=out, in_=in0, func=ACT.Copy, scale=factor)
@@ -213,15 +221,16 @@ def tile_fr_pb_t_kernel(
                 return
             unit, i, b = place(job)
             n = unit // HALVES
-            other, own = raw[unit, "x%d" % (1 - i)], raw[unit, "x%d" % i]
-            wide[unit, i, "other"] = wide_pool.tile([P, SLOTS, HALF], F32, name="wide_other%d" % i)
-            wide[unit, i, "gated"] = wide_pool.tile([P, SLOTS, HALF], F32, name="wide_gated%d" % i)
-            first = job == 0
-            size = HALF // 2 if first else HALF
-            for start in range(0, HALF, size):
-                columns = slice(start, start + size)
-                widen(wide[unit, i, "other"], other, columns)
-                gate(wide[unit, i, "gated"], own, i, n, columns, on_scalar=first)
+            source, own = raw[unit, "x%d" % (1 - i)], raw[unit, "x%d" % i]
+            wide[unit, i, "other"] = other = new_wide("other%d" % i)
+            wide[unit, i, "gated"] = gated = new_wide("gated%d" % i)
+            if job == 0:
+                for pair in range(PAIRS):
+                    widen(other, source, pair)
+                    gate(gated, own, i, n, slice(pair, pair + 1), on_scalar=True)
+            else:
+                widen(other, source)
+                gate(gated, own, i, n, slice(0, PAIRS), on_scalar=False)
 
         def plain_slot(unit, i):
             return i == 0 or unit % 2 == 1
@@ -230,30 +239,27 @@ def tile_fr_pb_t_kernel(
             if not starts(job, GROUP):
                 return
             unit, i, b = place(job)
-            wide[unit, i, "extra"] = wide_pool.tile([P, SLOTS, HALF], F32, name="wide_extra%d" % i)
-            widen(
-                wide[unit, i, "extra"],
-                raw[unit, "fe%d" % i],
-                slice(0, HALF),
-                SLOTS - 1 if plain_slot(unit, i) else SLOTS,
-            )
+            wide[unit, i, "extra"] = new_wide("extra%d" % i)
+            slots = SLOTS - 1 if plain_slot(unit, i) else SLOTS
+            widen(wide[unit, i, "extra"], raw[unit, "fe%d" % i], slots=slots)
 
         def sum_by_position(bank, first, second, b, last=None):
-            columns = slice(b * BLOCK, (b + 1) * BLOCK)
-            for j in range(SLOTS):
+            pair, k = divmod(b, PAIR)
+            for j in reversed(range(SLOTS)):
                 nc.tensor.matmul(
                     bank[:, j, :],
-                    lhsT=first[:, j, columns],
+                    lhsT=first[:, j, pair, k],
                     rhs=ident_f32[:],
                     is_transpose=True,
-                    start=(j == 0),
+                    start=(j == SLOTS - 1),
                     stop=False,
                 )
             for j in range(SLOTS):
                 plain = last is not None and j == SLOTS - 1
+                source = by_block(last[:, j, :]) if plain else second[:, j]
                 nc.tensor.matmul(
                     bank[:, j, :],
-                    lhsT=(last if plain else second)[:, j, columns],
+                    lhsT=source[:, pair, k],
                     rhs=(ident_bf16 if plain else ident_f32)[:],
                     is_transpose=not plain,
                     start=False,
@@ -339,20 +345,24 @@ def tile_fr_pb_t_kernel(
             if not starts(job, PAIR):
                 return
             unit, i, b = place(job)
-            own_bank[job] = psum_one.tile([P, PAIR, CHANNELS], BF16, name="own_ps", tag="own")
-            for k in range(PAIR):
-                for j in range(SLOTS):
-                    nc.tensor.transpose(
-                        own_bank[job][:, k, j * P : (j + 1) * P],
-                        raw[unit, "x%d" % i][:, j, (b + k) * BLOCK : (b + k + 1) * BLOCK],
-                        ident_bf16[:],
-                    )
+            pair = b // PAIR
+            own_bank[job] = psum_one.tile([P, CHANNELS], F32, name="own_ps", tag="own")
+            for j in range(SLOTS):
+                words = raw[unit, "x%d" % i][:, j, :].bitcast(F32)
+                nc.tensor.transpose(
+                    own_bank[job][:, j * P : (j + 1) * P],
+                    words[:, pair * BLOCK : (pair + 1) * BLOCK],
+                    ident_f32[:],
+                )
 
         def own_copy(job):
             if not starts(job, PAIR):
                 return
-            own_tile[job] = own_pool.tile([P, PAIR, CHANNELS], BF16, name="own")
-            nc.scalar.copy(out=own_tile[job][:], in_=own_bank[job][:])
+            own_tile[job] = own_pool.tile([P, CHANNELS, PAIR], BF16, name="own")
+            nc.scalar.copy(
+                out=own_tile[job][:].rearrange("q c k -> q (c k)").bitcast(F32),
+                in_=own_bank[job][:],
+            )
 
         def sum_t(job):
             if not starts(job, 1):
@@ -370,7 +380,7 @@ def tile_fr_pb_t_kernel(
             co_tile[job] = co_pool.tile([P, CHANNELS], BF16, name="co")
             nc.vector.scalar_tensor_tensor(
                 out=co_tile[job][:],
-                in0=own_tile[job - job % PAIR][:, job % PAIR, :],
+                in0=own_tile[job - job % PAIR][:, :, job % PAIR],
                 scalar=s_tile[group][:, b : b + 1],
                 in1=t_bank[job],
                 op0=ALU.mult,
@@ -405,8 +415,10 @@ def tile_fr_pb_t_kernel(
                 .rearrange("q (w u) -> q w u", u=2)
             )
             nc.scalar.copy(
-                out=grouped_words[:, b * BLOCK : (b + PAIR) * BLOCK, :],
-                in_=back_bank[job][:].rearrange("q u w -> q w u"),
+                out=grouped_words[:, b * BLOCK : (b + PAIR) * BLOCK, :].rearrange(
+                    "q (w k) u -> q w k u", k=PAIR
+                ),
+                in_=back_bank[job][:].rearrange("q u (k w) -> q w k u", k=PAIR),
             )
 
         def quantise(job):
@@ -460,11 +472,6 @@ def tile_fr_pb_t_kernel(
                 turn_biases(t - 4)
                 widen_for_r(t + 10)
                 widen_extra(t + 6)
-                own_transposes(t - 2)
-                project(t - 21, 0, 0)
-                project(t - 21, 0, 1)
-                project(t - 23, 1, 0)
-                project(t - 23, 1, 1)
                 sum_r(t + 2)
                 find_max(t)
                 exp_a(t + 1)
@@ -473,6 +480,11 @@ def tile_fr_pb_t_kernel(
                 invert(t - 4)
                 divide(t - 5)
                 fuse(t - 7)
+                own_transposes(t - 2)
+                project(t - 21, 0, 0)
+                project(t - 21, 0, 1)
+                project(t - 23, 1, 0)
+                project(t - 23, 1, 1)
                 sum_t(t - 6)
                 back_transposes(t - 10)
                 back_copy(t - 11)

@@ -19,6 +19,8 @@ CHANNELS = 512
 POSITIONS = 1024
 OUT_CHANNELS = 128
 SLOTS = CHANNELS // P
+LAST = SLOTS - 1
+PLAIN = SLOTS - 2
 HALF = 512
 HALVES = POSITIONS // HALF
 BLOCK = 128
@@ -204,9 +206,9 @@ def tile_fr_pb_t_kernel(
                 out=out, in0=in0, scalar1=1.0, scalar2=0.0, op0=ALU.mult, op1=ALU.add
             )
 
-        def gate(tile, source, i, n, pairs, on_scalar):
+        def gate(tile, source, i, n, pairs, slots, on_scalar):
             column = IMAGES * i + n
-            for j in range(SLOTS):
+            for j in slots:
                 out, in0 = tile[:, j, pairs], by_block(source[:, j, :])[:, pairs]
                 factor = gates[:, j, column : column + 1]
                 if on_scalar:
@@ -227,51 +229,57 @@ def tile_fr_pb_t_kernel(
             if job == 0:
                 for pair in range(PAIRS):
                     widen(other, source, pair)
-                    gate(gated, own, i, n, slice(pair, pair + 1), on_scalar=True)
+                    gate(gated, own, i, n, slice(pair, pair + 1), range(SLOTS), on_scalar=True)
             else:
                 widen(other, source)
-                gate(gated, own, i, n, slice(0, PAIRS), on_scalar=False)
+                gate(gated, own, i, n, slice(0, PAIRS), range(LAST), on_scalar=False)
 
-        def plain_slot(unit, i):
+        def gate_last(job):
+            if not starts(job, GROUP) or job == 0:
+                return
+            unit, i, b = place(job)
+            own = raw[unit, "x%d" % i]
+            pairs = slice(0, PAIRS)
+            gate(wide[unit, i, "gated"], own, i, unit // HALVES, pairs, (LAST,), on_scalar=True)
+
+        def is_plain(unit, i):
             return i == 0 or unit % 2 == 1
 
         def widen_extra(job):
             if not starts(job, GROUP):
                 return
             unit, i, b = place(job)
-            wide[unit, i, "extra"] = new_wide("extra%d" % i)
-            slots = SLOTS - 1 if plain_slot(unit, i) else SLOTS
-            widen(wide[unit, i, "extra"], raw[unit, "fe%d" % i], slots=slots)
+            wide[unit, i, "extra"] = tile = new_wide("extra%d" % i)
+            source, other = raw[unit, "fe%d" % i], raw[unit, "x%d" % (1 - i)]
+            widen(tile, source, slots=PLAIN if is_plain(unit, i) else LAST)
+            nc.gpsimd.tensor_tensor(
+                out=tile[:, LAST],
+                in0=by_block(other[:, LAST, :]),
+                in1=by_block(source[:, LAST, :]),
+                op=ALU.add,
+            )
 
-        def sum_by_position(bank, first, second, b, last=None):
-            pair, k = divmod(b, PAIR)
-            for j in reversed(range(SLOTS)):
+        def add_by_position(bank, terms):
+            for at, (j, columns, plain) in enumerate(terms):
                 nc.tensor.matmul(
                     bank[:, j, :],
-                    lhsT=first[:, j, pair, k],
-                    rhs=ident_f32[:],
-                    is_transpose=True,
-                    start=(j == SLOTS - 1),
-                    stop=False,
-                )
-            for j in range(SLOTS):
-                plain = last is not None and j == SLOTS - 1
-                source = by_block(last[:, j, :]) if plain else second[:, j]
-                nc.tensor.matmul(
-                    bank[:, j, :],
-                    lhsT=source[:, pair, k],
+                    lhsT=columns,
                     rhs=(ident_bf16 if plain else ident_f32)[:],
                     is_transpose=not plain,
-                    start=False,
-                    stop=(j == SLOTS - 1),
+                    start=(at == 0),
+                    stop=(at == len(terms) - 1),
                 )
 
         def sum_r(job):
             if not starts(job, 1):
                 return
             unit, i, b = place(job)
-            bank = psum_r.tile([P, SLOTS, P], F32, name="r_ps", tag="r")
-            sum_by_position(bank, wide[unit, i, "gated"], wide[unit, i, "other"], b)
+            pair, k = divmod(b, PAIR)
+            gated, other = wide[unit, i, "gated"], wide[unit, i, "other"]
+            bank = psum_r.tile([P, SLOTS, P], F32, name="r_ps")
+            terms = [(j, gated[:, j, pair, k], False) for j in reversed(range(SLOTS))]
+            terms += [(j, other[:, j, pair, k], False) for j in range(SLOTS)]
+            add_by_position(bank, terms)
             r_bank[job] = bank[:].rearrange("q j c -> q (j c)")
 
         def exp_a(job):
@@ -368,9 +376,15 @@ def tile_fr_pb_t_kernel(
             if not starts(job, 1):
                 return
             unit, i, b = place(job)
+            pair, k = divmod(b, PAIR)
+            other, extra = wide[unit, i, "other"], wide[unit, i, "extra"]
             bank = psum_t.tile([P, SLOTS, P], F32, name="t_ps")
-            last = raw[unit, "fe%d" % i] if plain_slot(unit, i) else None
-            sum_by_position(bank, wide[unit, i, "other"], wide[unit, i, "extra"], b, last)
+            terms = [(j, other[:, j, pair, k], False) for j in reversed(range(LAST))]
+            for j in range(SLOTS):
+                plain = j == PLAIN and is_plain(unit, i)
+                source = by_block(raw[unit, "fe%d" % i][:, j, :]) if plain else extra[:, j]
+                terms.append((j, source[:, pair, k], plain))
+            add_by_position(bank, terms)
             t_bank[job] = bank[:].rearrange("q j c -> q (j c)")
 
         def fuse(job):
@@ -434,11 +448,16 @@ def tile_fr_pb_t_kernel(
                 in_=grouped_tile[job // GROUP][:].rearrange("q w t -> q (w t)"),
             )
 
+        def at_end(unit, w):
+            return unit == JOBS // UNIT - 1 and w == 1
+
         def project(job, w, g):
             if not starts(job, UNIT):
                 return
             unit = job // UNIT
-            if g == 0:
+            if g == 0 and at_end(unit, w):
+                po_bank[unit, w] = psum_r.tile([P, HALF], F32, name="r_ps")
+            elif g == 0:
                 po_bank[unit, w] = psum_one.tile([P, HALF], F32, name="po_ps", tag="own")
             nc.tensor.matmul_mx(
                 out=po_bank[unit, w][:],
@@ -456,13 +475,15 @@ def tile_fr_pb_t_kernel(
             unit = job // UNIT
             n, h = divmod(unit, HALVES)
             po = out_pool.tile([P, HALF], F32, name="po")
-            nc.scalar.activation(
-                out=po[:],
-                in_=po_bank[unit, w][:],
-                func=ACT.Identity,
-                bias=biases[:, w : w + 1],
-                scale=1.0,
-            )
+            bias = biases[:, w : w + 1]
+            if at_end(unit, w):
+                nc.vector.tensor_scalar(
+                    out=po[:], in0=po_bank[unit, w][:], scalar1=bias, scalar2=None, op0=ALU.add
+                )
+            else:
+                nc.scalar.activation(
+                    out=po[:], in_=po_bank[unit, w][:], func=ACT.Identity, bias=bias, scale=1.0
+                )
             nc.sync.dma_start(out=outs[w][n, :, h * HALF : (h + 1) * HALF], in_=po[:])
 
         with tc.manual_schedule():
@@ -492,3 +513,4 @@ def tile_fr_pb_t_kernel(
                 own_copy(t - 2)
                 add_bias_and_store(t - 21, 0)
                 add_bias_and_store(t - 23, 1)
+                gate_last(t + 6)

@@ -20,7 +20,6 @@ POSITIONS = 1024
 OUT_CHANNELS = 128
 SLOTS = CHANNELS // P
 LAST = SLOTS - 1
-PLAIN = SLOTS - 2
 HALF = 512
 HALVES = POSITIONS // HALF
 BLOCK = 128
@@ -79,15 +78,16 @@ def tile_fr_pb_t_kernel(
         psum_t = ctx.enter_context(tc.psum_pool(name="psum_t", bufs=2))
         psum_one = ctx.enter_context(tc.psum_pool(name="psum_one", bufs=1))
 
-        ident_f32 = const.tile([P, P], F32)
-        make_identity(nc, ident_f32[:])
-        ident_bf16 = const.tile([P, P], BF16)
-        make_identity(nc, ident_bf16[:])
-
         gate_rows = const.tile([P, CHANNELS], BF16)
-        nc.vector.memset(gate_rows[:], 0.0)
+        nc.gpsimd.memset(gate_rows[:].bitcast(I32), 0)
         nc.sync.dma_start(out=gate_rows[0:IMAGES, :], in_=g1)
         nc.sync.dma_start(out=gate_rows[IMAGES : 2 * IMAGES, :], in_=g2)
+
+        ident_bf16 = const.tile([P, P], BF16)
+        make_identity(nc, ident_bf16[:])
+        ident_f32 = const.tile([P, P], F32)
+        make_identity(nc, ident_f32[:])
+
         gate_sorted = const.tile([P, SLOTS, P], BF16)
         rows_view = gate_rows[:].rearrange(
             "r (j0 pp j1 e) -> r j0 j1 pp e", j0=2, pp=P // 2, j1=2, e=2
@@ -245,13 +245,18 @@ def tile_fr_pb_t_kernel(
         def is_plain(unit, i):
             return i == 0 or unit % 2 == 1
 
+        def is_summed(i):
+            return i == 1
+
         def widen_extra(job):
             if not starts(job, GROUP):
                 return
             unit, i, b = place(job)
             wide[unit, i, "extra"] = tile = new_wide("extra%d" % i)
             source, other = raw[unit, "fe%d" % i], raw[unit, "x%d" % (1 - i)]
-            widen(tile, source, slots=PLAIN if is_plain(unit, i) else LAST)
+            widen(tile, source, slots=SLOTS - is_plain(unit, i) - is_summed(i))
+            if not is_summed(i):
+                return
             nc.gpsimd.tensor_tensor(
                 out=tile[:, LAST],
                 in0=by_block(other[:, LAST, :]),
@@ -378,10 +383,14 @@ def tile_fr_pb_t_kernel(
             unit, i, b = place(job)
             pair, k = divmod(b, PAIR)
             other, extra = wide[unit, i, "other"], wide[unit, i, "extra"]
-            bank = psum_t.tile([P, SLOTS, P], F32, name="t_ps")
-            terms = [(j, other[:, j, pair, k], False) for j in reversed(range(LAST))]
+            if job >= JOBS - GROUP:
+                bank = psum_r.tile([P, SLOTS, P], F32, name="r_ps")
+            else:
+                bank = psum_t.tile([P, SLOTS, P], F32, name="t_ps")
+            alone = SLOTS - is_summed(i)
+            terms = [(j, other[:, j, pair, k], False) for j in reversed(range(alone))]
             for j in range(SLOTS):
-                plain = j == PLAIN and is_plain(unit, i)
+                plain = j == alone - 1 and is_plain(unit, i)
                 source = by_block(raw[unit, "fe%d" % i][:, j, :]) if plain else extra[:, j]
                 terms.append((j, source[:, pair, k], plain))
             add_by_position(bank, terms)
@@ -404,7 +413,10 @@ def tile_fr_pb_t_kernel(
         def back_transposes(job):
             if not starts(job, PAIR):
                 return
-            back_bank[job] = psum_one.tile([P, 2, PAIR * BLOCK], F32, name="back_ps", tag="back")
+            if job == JOBS - PAIR:
+                back_bank[job] = psum_t.tile([P, 2, PAIR * BLOCK], F32, name="t_ps")
+            else:
+                back_bank[job] = psum_one.tile([P, 2, PAIR * BLOCK], F32, name="back_ps", tag="back")
             for k in range(PAIR):
                 co_words = co_tile[job + k][:].bitcast(F32)
                 for u in range(2):

@@ -245,8 +245,8 @@ def tile_fr_pb_t_kernel(
         def is_plain(unit, i):
             return i == 0 or unit % 2 == 1
 
-        def is_summed(i):
-            return i == 1
+        def summed(i):
+            return 2 * i
 
         def widen_extra(job):
             if not starts(job, GROUP):
@@ -254,13 +254,14 @@ def tile_fr_pb_t_kernel(
             unit, i, b = place(job)
             wide[unit, i, "extra"] = tile = new_wide("extra%d" % i)
             source, other = raw[unit, "fe%d" % i], raw[unit, "x%d" % (1 - i)]
-            widen(tile, source, slots=SLOTS - is_plain(unit, i) - is_summed(i))
-            if not is_summed(i):
+            widen(tile, source, slots=SLOTS - is_plain(unit, i) - summed(i))
+            first = SLOTS - summed(i)
+            if first == SLOTS:
                 return
             nc.gpsimd.tensor_tensor(
-                out=tile[:, LAST],
-                in0=by_block(other[:, LAST, :]),
-                in1=by_block(source[:, LAST, :]),
+                out=tile[:, first:].rearrange("p j h k w -> p (j h) k w"),
+                in0=by_block(other[:, first:, :].rearrange("p j s -> p (j s)")),
+                in1=by_block(source[:, first:, :].rearrange("p j s -> p (j s)")),
                 op=ALU.add,
             )
 
@@ -387,7 +388,7 @@ def tile_fr_pb_t_kernel(
                 bank = psum_r.tile([P, SLOTS, P], F32, name="r_ps")
             else:
                 bank = psum_t.tile([P, SLOTS, P], F32, name="t_ps")
-            alone = SLOTS - is_summed(i)
+            alone = SLOTS - summed(i)
             terms = [(j, other[:, j, pair, k], False) for j in reversed(range(alone))]
             for j in range(SLOTS):
                 plain = j == alone - 1 and is_plain(unit, i)

from contextlib import ExitStack

import concourse.mybir as mybir
from concourse.masks import make_identity

F32 = mybir.dt.float32
BF16 = mybir.dt.bfloat16
I32 = mybir.dt.int32
U32 = mybir.dt.uint32
U8 = mybir.dt.uint8
FP8X4 = mybir.dt.float8_e4m3fn_x4
ACT = mybir.ActivationFunctionType
ALU = mybir.AluOpType
AXIS = mybir.AxisListType

P = 128
IMAGES = 6
CHANNELS = 512
POSITIONS = 1024
OUT_CHANNELS = 128
SLOTS = CHANNELS // P
LAST = SLOTS - 1
HALF = 512
HALVES = POSITIONS // HALF
BLOCK = 128
BLOCKS = HALF // BLOCK
PAIR = 2
PAIRS = BLOCKS // PAIR
GROUP = BLOCKS
UNIT = 2 * GROUP
JOBS = IMAGES * HALVES * UNIT

FLOPS = 2 * IMAGES * POSITIONS * (2 * CHANNELS) * (2 * OUT_CHANNELS)


def tile_fr_pb_t_kernel(
    tc,
    x1,
    x2,
    FE_x1,
    FE_x2,
    g1,
    g2,
    p1_w_words,
    p1_w_scales,
    p1_b,
    p2_w_words,
    p2_w_scales,
    p2_b,
    out_0,
    out_1,
):
    nc = tc.nc

    def by_channel(feature_map):
        return feature_map.rearrange(
            "n (j0 pp j1 e) h w -> n j0 j1 pp e (h w)", j0=2, pp=P // 2, j1=2, e=2
        )

    streams = (by_channel(x1), by_channel(x2))
    extras = (by_channel(FE_x1), by_channel(FE_x2))
    outs = (
        out_0.rearrange("n o h w -> n o (h w)"),
        out_1.rearrange("n o h w -> n o (h w)"),
    )

    with ExitStack() as ctx:
        const = ctx.enter_context(tc.tile_pool(name="const", bufs=1))
        raw_pool = ctx.enter_context(tc.tile_pool(name="raw", bufs=3))
        wide_pool = ctx.enter_context(tc.tile_pool(name="wide", bufs=2))
        work = ctx.enter_context(tc.tile_pool(name="work", bufs=3))
        small = ctx.enter_context(tc.tile_pool(name="small", bufs=4))
        mx_pool = ctx.enter_context(tc.tile_pool(name="mx", bufs=2))
        out_pool = ctx.enter_context(tc.tile_pool(name="outp", bufs=4))
        co_pool = ctx.enter_context(tc.tile_pool(name="co", bufs=6))
        own_pool = ctx.enter_context(tc.tile_pool(name="own", bufs=5))
        psum_r = ctx.enter_context(tc.psum_pool(name="psum_r", bufs=4))
        psum_t = ctx.enter_context(tc.psum_pool(name="psum_t", bufs=2))
        psum_one = ctx.enter_context(tc.psum_pool(name="psum_one", bufs=1))

        gate_rows = const.tile([P, CHANNELS], BF16)
        nc.gpsimd.memset(gate_rows[:].bitcast(I32), 0)
        nc.sync.dma_start(out=gate_rows[0:IMAGES, :], in_=g1)
        nc.sync.dma_start(out=gate_rows[IMAGES : 2 * IMAGES, :], in_=g2)

        ident_bf16 = const.tile([P, P], BF16)
        make_identity(nc, ident_bf16[:])
        ident_f32 = const.tile([P, P], F32)
        make_identity(nc, ident_f32[:])

        gate_sorted = const.tile([P, SLOTS, P], BF16)
        rows_view = gate_rows[:].rearrange(
            "r (j0 pp j1 e) -> r j0 j1 pp e", j0=2, pp=P // 2, j1=2, e=2
        )
        for j in range(SLOTS):
            nc.vector.tensor_copy(
                out=gate_sorted[:, j, :].rearrange("r (pp e) -> r pp e", e=2),
                in_=rows_view[:, j % 2, j // 2],
            )
        gate_ps = psum_one.tile([P, SLOTS, P], BF16, tag="own")
        for j in range(SLOTS):
            nc.tensor.transpose(gate_ps[:, j, :], gate_sorted[:, j, :], ident_bf16[:])
        gates = const.tile([P, SLOTS, 2 * IMAGES], F32)
        nc.scalar.activation(
            out=gates[:], in_=gate_ps[:, :, 0 : 2 * IMAGES], func=ACT.Tanh, scale=0.5
        )
        nc.vector.tensor_scalar(
            out=gates[:], in0=gates[:], scalar1=0.5, scalar2=0.5, op0=ALU.mult, op1=ALU.add
        )

        bias_rows = const.tile([P, P], BF16)
        nc.vector.memset(bias_rows[:], 0.0)
        biases = const.tile([P, 2], F32)

        w_words = const.tile([P, 2, 2, OUT_CHANNELS], U32, align_bytes=64)
        w_scales = const.tile([P, 2, 2, OUT_CHANNELS], U8, align_bytes=64)
        nc.vector.memset(w_scales[:].bitcast(I32), 0)

        def load_weights(job):
            if job != 0:
                return
            nc.sync.dma_start(out=bias_rows[0:1, :], in_=p1_b.rearrange("(r o) -> r o", r=1))
            nc.sync.dma_start(out=bias_rows[1:2, :], in_=p2_b.rearrange("(r o) -> r o", r=1))
            for w, (words, scales) in enumerate(
                ((p1_w_words, p1_w_scales), (p2_w_words, p2_w_scales))
            ):
                nc.sync.dma_start(
                    out=w_words[:, w].bitcast(I32),
                    in_=words.rearrange("g p n t -> p g (n t)").bitcast(I32),
                )
                for quadrant in range(4):
                    nc.sync.dma_start(
                        out=w_scales[32 * quadrant : 32 * quadrant + 4, w].bitcast(I32),
                        in_=scales[:, 4 * quadrant : 4 * quadrant + 4, :]
                        .rearrange("g q n -> q g n")
                        .bitcast(I32),
                    )

        def turn_biases(job):
            if job != 0:
                return
            bias_ps = psum_one.tile([P, P], BF16, name="bias_ps", tag="back")
            nc.tensor.transpose(bias_ps[:], bias_rows[:], ident_bf16[:])
            nc.vector.tensor_copy(out=biases[:], in_=bias_ps[:, 0:2])

        raw = {}
        wide = {}
        r_bank = {}
        a_tile = {}
        minus_max = {}
        e_tile = {}
        sums = {}
        one_over = {}
        s_tile = {}
        own_bank = {}
        own_tile = {}
        t_bank = {}
        co_tile = {}
        back_bank = {}
        grouped_tile = {}
        re_codes = {}
        re_scales = {}
        po_bank = {}

        def starts(job, size):
            return 0 <= job < JOBS and job % size == 0

        def place(job):
            group, b = divmod(job, GROUP)
            unit, i = divmod(group, 2)
            return unit, i, b

        def load_unit(job):
            if not starts(job, UNIT):
                return
            unit = job // UNIT
            n, h = divmod(unit, HALVES)
            for name, view in (
                ("x1", streams[1]),
                ("x0", streams[0]),
                ("fe0", extras[0]),
                ("fe1", extras[1]),
            ):
                tile = raw_pool.tile([P, SLOTS, HALF], BF16, name="raw_" + name)
                for j in range(SLOTS):
                    nc.sync.dma_start(
                        out=tile[:, j, :],
                        in_=view[n, j % 2, j // 2, :, :, h * HALF : (h + 1) * HALF],
                    )
                raw[unit, name] = tile

        def by_block(row):
            return row.rearrange("p (h w k) -> p h k w", w=BLOCK, k=PAIR)

        def new_wide(name):
            return wide_pool.tile([P, SLOTS, PAIRS, PAIR, BLOCK], F32, name="wide_" + name)

        def widen(tile, source, pair=None, slots=SLOTS):
            if pair is None:
                out = tile[:, 0:slots].rearrange("p j h k w -> p (j h) k w")
                in0 = by_block(source[:, 0:slots].rearrange("p j s -> p (j s)"))
            else:
                out = tile[:, :, pair]
                in0 = source[:].rearrange("p j (h w k) -> p j h k w", w=BLOCK, k=PAIR)[:, :, pair]
            nc.gpsimd.tensor_scalar(
                out=out, in0=in0, scalar1=1.0, scalar2=0.0, op0=ALU.mult, op1=ALU.add
            )

        def gate(tile, source, i, n, pairs, slots, on_scalar):
            column = IMAGES * i + n
            for j in slots:
                out, in0 = tile[:, j, pairs], by_block(source[:, j, :])[:, pairs]
                factor = gates[:, j, column : column + 1]
                if on_scalar:
                    nc.scalar.activation(out=out, in_=in0, func=ACT.Copy, scale=factor)
                else:
                    nc.gpsimd.tensor_scalar(
                        out=out, in0=in0, scalar1=factor, scalar2=0.0, op0=ALU.mult, op1=ALU.add
                    )

        def widen_for_r(job):
            if not starts(job, GROUP):
                return
            unit, i, b = place(job)
            n = unit // HALVES
            source, own = raw[unit, "x%d" % (1 - i)], raw[unit, "x%d" % i]
            wide[unit, i, "other"] = other = new_wide("other%d" % i)
            wide[unit, i, "gated"] = gated = new_wide("gated%d" % i)
            if job == 0:
                for pair in range(PAIRS):
                    widen(other, source, pair)
                    gate(gated, own, i, n, slice(pair, pair + 1), range(SLOTS), on_scalar=True)
            else:
                widen(other, source)
                gate(gated, own, i, n, slice(0, PAIRS), range(LAST), on_scalar=False)

        def gate_last(job):
            if not starts(job, GROUP) or job == 0:
                return
            unit, i, b = place(job)
            own = raw[unit, "x%d" % i]
            pairs = slice(0, PAIRS)
            gate(wide[unit, i, "gated"], own, i, unit // HALVES, pairs, (LAST,), on_scalar=True)

        def is_plain(unit, i):
            return i == 0 or unit % 2 == 1

        def summed(i):
            return 2 * i

        def widen_extra(job):
            if not starts(job, GROUP):
                return
            unit, i, b = place(job)
            wide[unit, i, "extra"] = tile = new_wide("extra%d" % i)
            source, other = raw[unit, "fe%d" % i], raw[unit, "x%d" % (1 - i)]
            widen(tile, source, slots=SLOTS - is_plain(unit, i) - summed(i))
            first = SLOTS - summed(i)
            if first == SLOTS:
                return
            nc.gpsimd.tensor_tensor(
                out=tile[:, first:].rearrange("p j h k w -> p (j h) k w"),
                in0=by_block(other[:, first:, :].rearrange("p j s -> p (j s)")),
                in1=by_block(source[:, first:, :].rearrange("p j s -> p (j s)")),
                op=ALU.add,
            )

        def add_by_position(bank, terms):
            for at, (j, columns, plain) in enumerate(terms):
                nc.tensor.matmul(
                    bank[:, j, :],
                    lhsT=columns,
                    rhs=(ident_bf16 if plain else ident_f32)[:],
                    is_transpose=not plain,
                    start=(at == 0),
                    stop=(at == len(terms) - 1),
                )

        def sum_r(job):
            if not starts(job, 1):
                return
            unit, i, b = place(job)
            pair, k = divmod(b, PAIR)
            gated, other = wide[unit, i, "gated"], wide[unit, i, "other"]
            bank = psum_r.tile([P, SLOTS, P], F32, name="r_ps")
            terms = [(j, gated[:, j, pair, k], False) for j in reversed(range(SLOTS))]
            terms += [(j, other[:, j, pair, k], False) for j in range(SLOTS)]
            add_by_position(bank, terms)
            r_bank[job] = bank[:].rearrange("q j c -> q (j c)")

        def exp_a(job):
            if not starts(job, 1):
                return
            a_tile[job] = work.tile([P, CHANNELS], F32, name="a")
            nc.scalar.activation(out=a_tile[job][:], in_=r_bank[job], func=ACT.Exp)

        def find_max(job):
            if not starts(job, 1):
                return
            minus_max[job] = small.tile([P, 1], F32, name="minus_max")
            nc.vector.tensor_reduce(
                out=minus_max[job][:], in_=a_tile[job][:], axis=AXIS.X, op=ALU.max, negate=True
            )

        def exp_e(job):
            if not starts(job, 1):
                return
            group, b = divmod(job, GROUP)
            if b == 0:
                sums[group, "e"] = small.tile([P, GROUP], F32, name="sum_e")
            e_tile[job] = work.tile([P, CHANNELS], F32, name="e")
            nc.scalar.activation(
                out=e_tile[job][:],
                in_=a_tile[job][:],
                func=ACT.Exp,
                bias=minus_max[job][:, 0:1],
                scale=1.0,
                accum_out=sums[group, "e"][:, b : b + 1],
            )

        def invert(job):
            if not starts(job, GROUP):
                return
            group = job // GROUP
            one_over[group] = small.tile([P, GROUP], F32, name="one_over")
            nc.vector.reciprocal(out=one_over[group][:], in_=sums[group, "e"][:])

        def divide(job):
            if not starts(job, 1):
                return
            group, b = divmod(job, GROUP)
            if b == 0:
                s_tile[group] = small.tile([P, GROUP], F32, name="s")
            nc.scalar.activation(
                out=s_tile[group][:, b : b + 1],
                in_=sums[group, "er"][:, b : b + 1],
                func=ACT.Copy,
                scale=one_over[group][:, b : b + 1],
            )

        def sum_er(job):
            if not starts(job, 1):
                return
            group, b = divmod(job, GROUP)
            if b == 0:
                sums[group, "er"] = small.tile([P, GROUP], F32, name="sum_er")
            products = work.tile([P, CHANNELS], BF16, name="products")
            nc.vector.scalar_tensor_tensor(
                out=products[:],
                in0=e_tile[job][:],
                scalar=1.0,
                in1=r_bank[job],
                op0=ALU.mult,
                op1=ALU.mult,
                accum_out=sums[group, "er"][:, b : b + 1],
            )

        def own_transposes(job):
            if not starts(job, PAIR):
                return
            unit, i, b = place(job)
            pair = b // PAIR
            own_bank[job] = psum_one.tile([P, CHANNELS], F32, name="own_ps", tag="own")
            for j in range(SLOTS):
                words = raw[unit, "x%d" % i][:, j, :].bitcast(F32)
                nc.tensor.transpose(
                    own_bank[job][:, j * P : (j + 1) * P],
                    words[:, pair * BLOCK : (pair + 1) * BLOCK],
                    ident_f32[:],
                )

        def own_copy(job):
            if not starts(job, PAIR):
                return
            own_tile[job] = own_pool.tile([P, CHANNELS, PAIR], BF16, name="own")
            nc.scalar.copy(
                out=own_tile[job][:].rearrange("q c k -> q (c k)").bitcast(F32),
                in_=own_bank[job][:],
            )

        def sum_t(job):
            if not starts(job, 1):
                return
            unit, i, b = place(job)
            pair, k = divmod(b, PAIR)
            other, extra = wide[unit, i, "other"], wide[unit, i, "extra"]
            if job >= JOBS - GROUP:
                bank = psum_r.tile([P, SLOTS, P], F32, name="r_ps")
            else:
                bank = psum_t.tile([P, SLOTS, P], F32, name="t_ps")
            alone = SLOTS - summed(i)
            terms = [(j, other[:, j, pair, k], False) for j in reversed(range(alone))]
            for j in range(SLOTS):
                plain = j == alone - 1 and is_plain(unit, i)
                source = by_block(raw[unit, "fe%d" % i][:, j, :]) if plain else extra[:, j]
                terms.append((j, source[:, pair, k], plain))
            add_by_position(bank, terms)
            t_bank[job] = bank[:].rearrange("q j c -> q (j c)")

        def fuse(job):
            if not starts(job, 1):
                return
            group, b = divmod(job, GROUP)
            co_tile[job] = co_pool.tile([P, CHANNELS], BF16, name="co")
            nc.vector.scalar_tensor_tensor(
                out=co_tile[job][:],
                in0=own_tile[job - job % PAIR][:, :, job % PAIR],
                scalar=s_tile[group][:, b : b + 1],
                in1=t_bank[job],
                op0=ALU.mult,
                op1=ALU.add,
            )

        def back_transposes(job):
            if not starts(job, PAIR):
                return
            if job == JOBS - PAIR:
                back_bank[job] = psum_t.tile([P, 2, PAIR * BLOCK], F32, name="t_ps")
            else:
                back_bank[job] = psum_one.tile([P, 2, PAIR * BLOCK], F32, name="back_ps", tag="back")
            for k in range(PAIR):
                co_words = co_tile[job + k][:].bitcast(F32)
                for u in range(2):
                    nc.tensor.transpose(
                        back_bank[job][:, u, k * BLOCK : (k + 1) * BLOCK],
                        co_words[:, u * P : (u + 1) * P],
                        ident_f32[:],
                    )

        def back_copy(job):
            if not starts(job, PAIR):
                return
            group, b = divmod(job, GROUP)
            if b == 0:
                grouped_tile[group] = mx_pool.tile(
                    [P, HALF, SLOTS], BF16, name="grouped", align_bytes=64
                )
            grouped_words = (
                grouped_tile[group][:]
                .rearrange("q w t -> q (w t)")
                .bitcast(F32)
                .rearrange("q (w u) -> q w u", u=2)
            )
            nc.scalar.copy(
                out=grouped_words[:, b * BLOCK : (b + PAIR) * BLOCK, :].rearrange(
                    "q (w k) u -> q w k u", k=PAIR
                ),
                in_=back_bank[job][:].rearrange("q u (k w) -> q w k u", k=PAIR),
            )

        def quantise(job):
            if not starts(job, GROUP):
                return
            unit, i, b = place(job)
            if i == 0:
                re_codes[unit] = mx_pool.tile([P, 2, HALF], U32, name="re_codes", align_bytes=64)
                re_scales[unit] = mx_pool.tile([P, 2, HALF], U8, name="re_scales", align_bytes=64)
            nc.vector.quantize_mx(
                out=re_codes[unit][:, i, :].bitcast(FP8X4),
                scales=re_scales[unit][:, i, :],
                in_=grouped_tile[job // GROUP][:].rearrange("q w t -> q (w t)"),
            )

        def at_end(unit, w):
            return unit == JOBS // UNIT - 1 and w == 1

        def project(job, w, g):
            if not starts(job, UNIT):
                return
            unit = job // UNIT
            if g == 0 and at_end(unit, w):
                po_bank[unit, w] = psum_r.tile([P, HALF], F32, name="r_ps")
            elif g == 0:
                po_bank[unit, w] = psum_one.tile([P, HALF], F32, name="po_ps", tag="own")
            nc.tensor.matmul_mx(
                out=po_bank[unit, w][:],
                lhsT=w_words[:, w, g, :].bitcast(FP8X4),
                lhsT_scale=w_scales[:, w, g, :],
                rhs=re_codes[unit][:, g, :].bitcast(FP8X4),
                rhs_scale=re_scales[unit][:, g, :],
                start=(g == 0),
                stop=(g == 1),
            )

        def add_bias_and_store(job, w):
            if not starts(job, UNIT):
                return
            unit = job // UNIT
            n, h = divmod(unit, HALVES)
            po = out_pool.tile([P, HALF], F32, name="po")
            bias = biases[:, w : w + 1]
            if at_end(unit, w):
                nc.vector.tensor_scalar(
                    out=po[:], in0=po_bank[unit, w][:], scalar1=bias, scalar2=None, op0=ALU.add
                )
            else:
                nc.scalar.activation(
                    out=po[:], in_=po_bank[unit, w][:], func=ACT.Identity, bias=bias, scale=1.0
                )
            nc.sync.dma_start(out=outs[w][n, :, h * HALF : (h + 1) * HALF], in_=po[:])

        with tc.manual_schedule():
            for t in range(-16, JOBS + 27):
                load_unit(t + 16)
                load_weights(t + 15)
                turn_biases(t - 4)
                widen_for_r(t + 10)
                widen_extra(t + 6)
                sum_r(t + 2)
                find_max(t)
                exp_a(t + 1)
                exp_e(t)
                sum_er(t - 1)
                invert(t - 4)
                divide(t - 5)
                fuse(t - 7)
                own_transposes(t - 2)
                project(t - 21, 0, 0)
                project(t - 21, 0, 1)
                project(t - 23, 1, 0)
                project(t - 23, 1, 1)
                sum_t(t - 6)
                back_transposes(t - 10)
                back_copy(t - 11)
                quantise(t - 15)
                own_copy(t - 2)
                add_bias_and_store(t - 21, 0)
                add_bias_and_store(t - 23, 1)
                gate_last(t + 6)
